import numpy as np
import ml_dtypes


def mxq(x, axis, fmt="e4m3"):
    dtype, down = {"e4m3": (ml_dtypes.float8_e4m3fn, 7), "e5m2": (ml_dtypes.float8_e5m2, 14)}[fmt]
    v = np.moveaxis(np.asarray(x, np.float32).astype(ml_dtypes.bfloat16).astype(np.float64), axis, -1)
    blocks = v.reshape(v.shape[:-1] + (-1, 32))
    amax = np.abs(blocks).max(-1, keepdims=True)
    byte = np.maximum(np.where(amax > 0, np.frexp(amax)[1] - 1 + 127, 0) - down, 1)
    scale = np.exp2(byte - 127.0)
    codes = (blocks / scale).astype(np.float32).astype(dtype).astype(np.float64)
    return np.moveaxis((codes * scale).reshape(v.shape), -1, axis)


WIDE = False


def mx_kscale(k):
    if not WIDE:
        return np.ones(k)
    levels = np.array([10, -10, 5, -5, 0])
    a = np.random.permutation(np.resize(levels, k // 512 * 4)).reshape(k // 512, 4)
    idx = np.arange(k)
    return np.exp2(a[idx // 512, idx % 128 // 32])


BF16 = ml_dtypes.bfloat16


def bf(x):
    return np.asarray(x, np.float32).astype(BF16)


def f64(x):
    return np.asarray(x).astype(np.float64)


B, T, H, D = 32, 128, 2, 1024
A = 1.5 / D ** 0.25


def relative_shift(x):
    b, h, t, tt = x.shape
    x = np.pad(x, [[0, 0], [0, 0], [0, 0], [1, 0]])
    x = x.reshape(b, h, tt + 1, t)[:, :, 1:, :]
    return x.reshape(b, h, t, tt)


def setup_inputs():
    s = mx_kscale(D)
    return {"q": bf(np.random.standard_normal((B, T, H, D)) * A * s),
            "k": bf(np.random.standard_normal((B, T, H, D)) * A / s),
            "r_w_bias": bf(np.random.standard_normal((H, D)) * 0.5 * A * s),
            "r_r_bias": bf(np.random.standard_normal((H, D)) * 0.5 * A * s),
            "rel_pos_emb": bf(np.random.standard_normal((T, H, D)) * A / s)}


def reference(q, k, r_w_bias, r_r_bias, rel_pos_emb):
    qw = (f64(q) + f64(r_w_bias)).transpose(0, 2, 1, 3)
    qr = (f64(q) + f64(r_r_bias)).transpose(0, 2, 1, 3)
    kt = f64(k).transpose(0, 2, 3, 1)
    rt = f64(rel_pos_emb).transpose(1, 2, 0)
    content = mxq(qw, 3, "e4m3") @ mxq(kt, 2, "e4m3")
    rel = mxq(qr, 3, "e4m3") @ mxq(rt, 1, "e4m3")
    return content + relative_shift(rel)

@@ -1,0 +1,214 @@
+from contextlib import ExitStack
+
+import concourse.mybir as mybir
+from concourse.masks import make_identity
+
+F32 = mybir.dt.float32
+BF16 = mybir.dt.bfloat16
+U32 = mybir.dt.uint32
+U8 = mybir.dt.uint8
+FP8X4 = mybir.dt.float8_e4m3fn_x4
+ADD = mybir.AluOpType.add
+
+B, T, H, D = 32, 128, 2, 1024
+P = 128
+FLOPS = 2 * 2 * B * H * T * T * D
+
+GROUP = 4
+NGROUPS = B * H // GROUP
+SLOT = (T + 1) * T
+LAG = 2
+NSTG = 4
+
+
+def transpose_head(nc, bank, words, ident):
+    for u in range(2):
+        for g in range(2):
+            c = 2 * u + g
+            src = 256 * g + 128 * u
+            nc.tensor.transpose(bank[:, 128 * c : 128 * c + 128], words[:, src : src + 128], ident)
+
+
+def leave_bank(nc, dst_words, bank):
+    nc.scalar.copy(
+        out=dst_words.rearrange("p (x u) -> p x u", u=2),
+        in_=bank[:].rearrange("p (u x) -> p x u", u=2),
+    )
+
+
+def tile_relativepositionembedding_pa_t_kernel(tc, q, k, r_w_bias, r_r_bias, rel_pos_emb, out):
+    nc = tc.nc
+    out_flat = out.rearrange("b h t j -> (b h t j)")
+    with ExitStack() as ctx:
+        const = ctx.enter_context(tc.tile_pool(name="const", bufs=1))
+        io = ctx.enter_context(tc.tile_pool(name="io", bufs=5))
+        work = ctx.enter_context(tc.tile_pool(name="work", bufs=3))
+        codes = ctx.enter_context(tc.tile_pool(name="codes", bufs=2 * LAG + 3))
+        back_pool = ctx.enter_context(tc.tile_pool(name="backp", bufs=LAG + 2))
+        psum = ctx.enter_context(tc.psum_pool(name="psum", bufs=2))
+
+        ident = const.tile([P, P], F32)
+        make_identity(nc, ident[:])
+
+        brow = const.tile([P, D], BF16)
+        nc.vector.memset(brow[:], 0.0)
+        nc.sync.dma_start(out=brow[0:2, :], in_=r_w_bias)
+        nc.sync.dma_start(out=brow[2:4, :], in_=r_r_bias)
+        rsb = const.tile([P, H * D], BF16)
+
+        stg = []
+        for s in range(NSTG):
+            st = const.tile([P, GROUP * (T + 1)], F32, name="stg%d" % s)
+            nc.vector.memset(st[:], 0.0)
+            stg.append(st)
+
+        pb = psum.tile([P, 512], F32, tag="xq")
+        brow_w = brow[:].bitcast(F32)
+        for c in range(4):
+            nc.tensor.transpose(pb[:, 128 * c : 128 * c + 128], brow_w[:, 128 * c : 128 * c + 128], ident[:])
+        bsm = const.tile([P, 16], F32)
+        nc.vector.tensor_copy(
+            out=bsm[:].rearrange("p (i c) -> p i c", c=4),
+            in_=pb[:].rearrange("p (c i) -> p i c", c=4)[:, 0:4, :],
+        )
+        bfull = const.tile([P, 4 * D], BF16, align_bytes=64)
+        bfull_w = bfull[:].bitcast(F32)
+        for i in range(4):
+            nc.vector.tensor_copy(
+                out=bfull_w[:, 512 * i : 512 * i + 512].rearrange("p (g r u) -> p g r u", g=2, u=2),
+                in_=bsm[:, 4 * i : 4 * i + 4].rearrange("p (g u) -> p g u", g=2).unsqueeze(2).to_broadcast([P, 2, T, 2]),
+            )
+
+        qts = {}
+        kts = {}
+
+        def load(b):
+            qt = io.tile([P, H * D], BF16, tag="q")
+            nc.sync.dma_start(out=qt[:], in_=q[b].rearrange("t h d -> t (h d)"))
+            kt = io.tile([P, H * D], BF16, tag="k")
+            nc.sync.dma_start(out=kt[:], in_=k[b].rearrange("t h d -> t (h d)"))
+            qts[b] = qt
+            kts[b] = kt
+
+        load(0)
+        nc.sync.dma_start(out=rsb[:], in_=rel_pos_emb.rearrange("j h d -> j (h d)"))
+
+        gr = const.tile([P, H * D], BF16, align_bytes=64)
+        gr_w = gr[:].bitcast(F32)
+        rsb_w = rsb[:].bitcast(F32)
+        for h in range(H):
+            xr = psum.tile([P, 512], F32, tag="xk")
+            transpose_head(nc, xr, rsb_w[:, 512 * h : 512 * h + 512], ident[:])
+            leave_bank(nc, gr_w[:, 512 * h : 512 * h + 512], xr)
+        rc = const.tile([P, 512], U32, align_bytes=64)
+        rs = const.tile([P, 512], U8, align_bytes=64)
+        nc.vector.quantize_mx(out=rc[:].bitcast(FP8X4), scales=rs[:], in_=gr[:])
+
+        qcs = {}
+        qss = {}
+        kcs = {}
+        kss = {}
+        rbs = {}
+        rels = {}
+
+        def front(b):
+            if b + 1 < B:
+                load(b + 1)
+            qw_ = qts[b][:].bitcast(F32)
+            kw_ = kts[b][:].bitcast(F32)
+            raw = work.tile([P, H * 512], F32, tag="raw")
+            gk = work.tile([P, H * D], BF16, tag="gk", align_bytes=64)
+            gk_w = gk[:].bitcast(F32)
+            for h in range(H):
+                xq = psum.tile([P, 512], F32, tag="xq")
+                transpose_head(nc, xq, qw_[:, 512 * h : 512 * h + 512], ident[:])
+                leave_bank(nc, raw[:, 512 * h : 512 * h + 512], xq)
+            for h in range(H):
+                xk = psum.tile([P, 512], F32, tag="xk")
+                transpose_head(nc, xk, kw_[:, 512 * h : 512 * h + 512], ident[:])
+                leave_bank(nc, gk_w[:, 512 * h : 512 * h + 512], xk)
+            gq = work.tile([P, 4 * D], BF16, tag="gq", align_bytes=64)
+            nc.vector.tensor_tensor(
+                out=gq[:].rearrange("p (w x) -> p w x", w=2),
+                in0=raw[:].bitcast(BF16).unsqueeze(1).to_broadcast([P, 2, H * D]),
+                in1=bfull[:].rearrange("p (w x) -> p w x", w=2),
+                op=ADD,
+            )
+            kc = codes.tile([P, 512], U32, tag="kc", align_bytes=64)
+            ks = codes.tile([P, 512], U8, tag="ks", align_bytes=64)
+            nc.vector.quantize_mx(out=kc[:].bitcast(FP8X4), scales=ks[:], in_=gk[:])
+            qc = codes.tile([P, 1024], U32, tag="qc", align_bytes=64)
+            qs = codes.tile([P, 1024], U8, tag="qs", align_bytes=64)
+            nc.vector.quantize_mx(out=qc[:].bitcast(FP8X4), scales=qs[:], in_=gq[:])
+            qcs[b], qss[b], kcs[b], kss[b] = qc, qs, kc, ks
+
+            gi = b // 2
+            if b % 2 == 0:
+                rel_new = psum.tile([P, 512], F32, tag="rel")
+                rels[gi] = rel_new
+            rel = rels[gi]
+            for h in range(H):
+                i = 2 * (b % 2) + h
+                for g in range(2):
+                    a = 128 * (2 * (2 + h) + g)
+                    r0 = 128 * (2 * h + g)
+                    nc.tensor.matmul_mx(
+                        out=rel[:, 128 * i : 128 * i + 128],
+                        lhsT=qc[:, a : a + 128].bitcast(FP8X4),
+                        lhsT_scale=qs[:, a : a + 128],
+                        rhs=rc[:, r0 : r0 + 128].bitcast(FP8X4),
+                        rhs_scale=rs[:, r0 : r0 + 128],
+                        start=(g == 0),
+                        stop=(g == 1),
+                    )
+
+        def shift_trip(gi):
+            st = stg[gi % NSTG]
+            nc.scalar.copy(
+                out=st[:].rearrange("p (i c) -> p i c", i=GROUP)[:, :, 1 : T + 1],
+                in_=rels[gi][:].rearrange("p (i j) -> p i j", i=GROUP),
+            )
+            base = min(GROUP * SLOT * gi, B * H * T * T - GROUP * SLOT)
+            area = out_flat[base : base + GROUP * SLOT]
+            nc.sync.dma_start(
+                out=area.rearrange("(i t c) -> t i c", i=GROUP, t=T),
+                in_=st[:].rearrange("p (i c) -> p i c", i=GROUP),
+            )
+            rb = back_pool.tile([P, GROUP * T], F32, tag="rb")
+            nc.sync.dma_start(
+                out=rb[:].rearrange("p (i j) -> p i j", i=GROUP),
+                in_=area.rearrange("(i f) -> i f", i=GROUP)[:, T:SLOT].rearrange("i (t j) -> t i j", t=T),
+            )
+            rbs[gi] = rb
+
+        def back(gi):
+            cont = psum.tile([P, 512], F32, tag="cont")
+            for i in range(GROUP):
+                b = 2 * gi + i // 2
+                h = i % 2
+                for g in range(2):
+                    a = 128 * (2 * h + g)
+                    nc.tensor.matmul_mx(
+                        out=cont[:, 128 * i : 128 * i + 128],
+                        lhsT=qcs[b][:, a : a + 128].bitcast(FP8X4),
+                        lhsT_scale=qss[b][:, a : a + 128],
+                        rhs=kcs[b][:, a : a + 128].bitcast(FP8X4),
+                        rhs_scale=kss[b][:, a : a + 128],
+                        start=(g == 0),
+                        stop=(g == 1),
+                    )
+            fin = back_pool.tile([P, GROUP * T], F32, tag="fin")
+            nc.vector.tensor_tensor(out=fin[:], in0=cont[:], in1=rbs[gi][:], op=ADD)
+            nc.sync.dma_start(
+                out=out[2 * gi : 2 * gi + 2].rearrange("b h t j -> t (b h) j"),
+                in_=fin[:].rearrange("p (i j) -> p i j", i=GROUP),
+            )
+
+        for gi in range(NGROUPS):
+            front(2 * gi)
+            front(2 * gi + 1)
+            shift_trip(gi)
+            if gi >= LAG:
+                back(gi - LAG)
+        for gi in range(NGROUPS - LAG, NGROUPS):
+            back(gi)

@@ -17,7 +17,8 @@ FLOPS = 2 * 2 * B * H * T * T * D
 GROUP = 4
 NGROUPS = B * H // GROUP
 SLOT = (T + 1) * T
-LAG = 2
+LAG = 3
+AHEAD = 2
 NSTG = 4
 
 
@@ -41,11 +42,14 @@ def tile_relativepositionembedding_pa_t_kernel(tc, q, k, r_w_bias, r_r_bias, rel
     out_flat = out.rearrange("b h t j -> (b h t j)")
     with ExitStack() as ctx:
         const = ctx.enter_context(tc.tile_pool(name="const", bufs=1))
-        io = ctx.enter_context(tc.tile_pool(name="io", bufs=5))
-        work = ctx.enter_context(tc.tile_pool(name="work", bufs=3))
-        codes = ctx.enter_context(tc.tile_pool(name="codes", bufs=2 * LAG + 3))
-        back_pool = ctx.enter_context(tc.tile_pool(name="backp", bufs=LAG + 2))
+        io = ctx.enter_context(tc.tile_pool(name="io", bufs=4))
+        rawp = ctx.enter_context(tc.tile_pool(name="rawp", bufs=LAG + AHEAD + 2))
+        gkp = ctx.enter_context(tc.tile_pool(name="gkp", bufs=AHEAD + 2))
+        work = ctx.enter_context(tc.tile_pool(name="work", bufs=2))
+        codes = ctx.enter_context(tc.tile_pool(name="codes", bufs=3))
+        back_pool = ctx.enter_context(tc.tile_pool(name="backp", bufs=4))
         psum = ctx.enter_context(tc.psum_pool(name="psum", bufs=2))
+        ctx.enter_context(tc.manual_schedule())
 
         ident = const.tile([P, P], F32)
         make_identity(nc, ident[:])
@@ -54,7 +58,26 @@ def tile_relativepositionembedding_pa_t_kernel(tc, q, k, r_w_bias, r_r_bias, rel
         nc.vector.memset(brow[:], 0.0)
         nc.sync.dma_start(out=brow[0:2, :], in_=r_w_bias)
         nc.sync.dma_start(out=brow[2:4, :], in_=r_r_bias)
+
+        qts = {}
+        kts = {}
+
+        def load_q(b):
+            if 0 <= b < B:
+                qt = io.tile([P, H * D], BF16, tag="q")
+                nc.sync.dma_start(out=qt[:], in_=q[b].rearrange("t h d -> t (h d)"))
+                qts[b] = qt
+
+        def load_k(b):
+            if 0 <= b < B:
+                kt = io.tile([P, H * D], BF16, tag="k")
+                nc.sync.dma_start(out=kt[:], in_=k[b].rearrange("t h d -> t (h d)"))
+                kts[b] = kt
+
+        load_q(0)
+        load_q(1)
         rsb = const.tile([P, H * D], BF16)
+        nc.sync.dma_start(out=rsb[:], in_=rel_pos_emb.rearrange("j h d -> j (h d)"))
 
         stg = []
         for s in range(NSTG):
@@ -62,7 +85,7 @@ def tile_relativepositionembedding_pa_t_kernel(tc, q, k, r_w_bias, r_r_bias, rel
             nc.vector.memset(st[:], 0.0)
             stg.append(st)
 
-        pb = psum.tile([P, 512], F32, tag="xq")
+        pb = psum.tile([P, 512], F32, tag="xk")
         brow_w = brow[:].bitcast(F32)
         for c in range(4):
             nc.tensor.transpose(pb[:, 128 * c : 128 * c + 128], brow_w[:, 128 * c : 128 * c + 128], ident[:])
@@ -73,142 +96,170 @@ def tile_relativepositionembedding_pa_t_kernel(tc, q, k, r_w_bias, r_r_bias, rel
         )
         bfull = const.tile([P, 4 * D], BF16, align_bytes=64)
         bfull_w = bfull[:].bitcast(F32)
-        for i in range(4):
+        for i in (2, 3, 0, 1):
             nc.vector.tensor_copy(
                 out=bfull_w[:, 512 * i : 512 * i + 512].rearrange("p (g r u) -> p g r u", g=2, u=2),
                 in_=bsm[:, 4 * i : 4 * i + 4].rearrange("p (g u) -> p g u", g=2).unsqueeze(2).to_broadcast([P, 2, T, 2]),
             )
 
-        qts = {}
-        kts = {}
-
-        def load(b):
-            qt = io.tile([P, H * D], BF16, tag="q")
-            nc.sync.dma_start(out=qt[:], in_=q[b].rearrange("t h d -> t (h d)"))
-            kt = io.tile([P, H * D], BF16, tag="k")
-            nc.sync.dma_start(out=kt[:], in_=k[b].rearrange("t h d -> t (h d)"))
-            qts[b] = qt
-            kts[b] = kt
-
-        load(0)
-        nc.sync.dma_start(out=rsb[:], in_=rel_pos_emb.rearrange("j h d -> j (h d)"))
-
         gr = const.tile([P, H * D], BF16, align_bytes=64)
-        gr_w = gr[:].bitcast(F32)
-        rsb_w = rsb[:].bitcast(F32)
-        for h in range(H):
-            xr = psum.tile([P, 512], F32, tag="xk")
-            transpose_head(nc, xr, rsb_w[:, 512 * h : 512 * h + 512], ident[:])
-            leave_bank(nc, gr_w[:, 512 * h : 512 * h + 512], xr)
         rc = const.tile([P, 512], U32, align_bytes=64)
         rs = const.tile([P, 512], U8, align_bytes=64)
-        nc.vector.quantize_mx(out=rc[:].bitcast(FP8X4), scales=rs[:], in_=gr[:])
 
-        qcs = {}
-        qss = {}
-        kcs = {}
-        kss = {}
-        rbs = {}
+        def prepare_r_tensor():
+            gr_w = gr[:].bitcast(F32)
+            rsb_w = rsb[:].bitcast(F32)
+            for h in range(H):
+                xr = psum.tile([P, 512], F32, tag="xk")
+                transpose_head(nc, xr, rsb_w[:, 512 * h : 512 * h + 512], ident[:])
+                leave_bank(nc, gr_w[:, 512 * h : 512 * h + 512], xr)
+
+        raws = {}
+        gks = {}
+        cod = {}
         rels = {}
+        conts = {}
+        rbs = {}
+        fins = {}
 
-        def front(b):
-            if b + 1 < B:
-                load(b + 1)
-            qw_ = qts[b][:].bitcast(F32)
-            kw_ = kts[b][:].bitcast(F32)
-            raw = work.tile([P, H * 512], F32, tag="raw")
-            gk = work.tile([P, H * D], BF16, tag="gk", align_bytes=64)
-            gk_w = gk[:].bitcast(F32)
+        def turn_q(b):
+            if not 0 <= b < B:
+                return
+            words = qts[b][:].bitcast(F32)
+            raw = rawp.tile([P, H * 512], F32, tag="raw")
             for h in range(H):
                 xq = psum.tile([P, 512], F32, tag="xq")
-                transpose_head(nc, xq, qw_[:, 512 * h : 512 * h + 512], ident[:])
+                transpose_head(nc, xq, words[:, 512 * h : 512 * h + 512], ident[:])
                 leave_bank(nc, raw[:, 512 * h : 512 * h + 512], xq)
+            raws[b] = raw
+
+        def turn_k(b):
+            if not 0 <= b < B:
+                return
+            words = kts[b][:].bitcast(F32)
+            gk = gkp.tile([P, H * D], BF16, tag="gk", align_bytes=64)
+            gk_w = gk[:].bitcast(F32)
             for h in range(H):
                 xk = psum.tile([P, 512], F32, tag="xk")
-                transpose_head(nc, xk, kw_[:, 512 * h : 512 * h + 512], ident[:])
+                transpose_head(nc, xk, words[:, 512 * h : 512 * h + 512], ident[:])
                 leave_bank(nc, gk_w[:, 512 * h : 512 * h + 512], xk)
-            gq = work.tile([P, 4 * D], BF16, tag="gq", align_bytes=64)
-            nc.vector.tensor_tensor(
-                out=gq[:].rearrange("p (w x) -> p w x", w=2),
-                in0=raw[:].bitcast(BF16).unsqueeze(1).to_broadcast([P, 2, H * D]),
-                in1=bfull[:].rearrange("p (w x) -> p w x", w=2),
-                op=ADD,
-            )
-            kc = codes.tile([P, 512], U32, tag="kc", align_bytes=64)
-            ks = codes.tile([P, 512], U8, tag="ks", align_bytes=64)
-            nc.vector.quantize_mx(out=kc[:].bitcast(FP8X4), scales=ks[:], in_=gk[:])
-            qc = codes.tile([P, 1024], U32, tag="qc", align_bytes=64)
-            qs = codes.tile([P, 1024], U8, tag="qs", align_bytes=64)
-            nc.vector.quantize_mx(out=qc[:].bitcast(FP8X4), scales=qs[:], in_=gq[:])
-            qcs[b], qss[b], kcs[b], kss[b] = qc, qs, kc, ks
+            gks[b] = gk
 
-            gi = b // 2
-            if b % 2 == 0:
-                rel_new = psum.tile([P, 512], F32, tag="rel")
-                rels[gi] = rel_new
-            rel = rels[gi]
+        def add_bias(b, w):
+            if not 0 <= b < B:
+                return None
+            g_ = work.tile([P, H * D], BF16, tag="g%d" % w, align_bytes=64)
+            nc.vector.tensor_tensor(
+                out=g_[:], in0=raws[b][:].bitcast(BF16), in1=bfull[:, 2 * D * w : 2 * D * w + 2 * D], op=ADD
+            )
+            return g_
+
+        def quantise(b, kind, src):
+            if src is None:
+                return
+            c_ = codes.tile([P, 512], U32, tag="c" + kind, align_bytes=64)
+            s_ = codes.tile([P, 512], U8, tag="s" + kind, align_bytes=64)
+            nc.vector.quantize_mx(out=c_[:].bitcast(FP8X4), scales=s_[:], in_=src[:])
+            cod[(kind, b)] = (c_, s_)
+
+        def multiply(bank, b, left, right):
+            lc, ls = left
+            mc, ms = right
             for h in range(H):
                 i = 2 * (b % 2) + h
                 for g in range(2):
-                    a = 128 * (2 * (2 + h) + g)
-                    r0 = 128 * (2 * h + g)
+                    a = 128 * (2 * h + g)
                     nc.tensor.matmul_mx(
-                        out=rel[:, 128 * i : 128 * i + 128],
-                        lhsT=qc[:, a : a + 128].bitcast(FP8X4),
-                        lhsT_scale=qs[:, a : a + 128],
-                        rhs=rc[:, r0 : r0 + 128].bitcast(FP8X4),
-                        rhs_scale=rs[:, r0 : r0 + 128],
+                        out=bank[:, 128 * i : 128 * i + 128],
+                        lhsT=lc[:, a : a + 128].bitcast(FP8X4),
+                        lhsT_scale=ls[:, a : a + 128],
+                        rhs=mc[:, a : a + 128].bitcast(FP8X4),
+                        rhs_scale=ms[:, a : a + 128],
                         start=(g == 0),
                         stop=(g == 1),
                     )
 
-        def shift_trip(gi):
+        def mult_rel(b):
+            if not 0 <= b < B:
+                return
+            if b % 2 == 0:
+                rel_new = psum.tile([P, 512], F32, tag="rel")
+                rels[b // 2] = rel_new
+            multiply(rels[b // 2], b, cod[("r", b)], (rc, rs))
+
+        def mult_content(b):
+            if not 0 <= b < B:
+                return
+            if b % 2 == 0:
+                cont_new = psum.tile([P, 512], F32, tag="cont")
+                conts[b // 2] = cont_new
+            multiply(conts[b // 2], b, cod[("w", b)], cod[("k", b)])
+
+        def area_of(gi):
+            base = min(GROUP * SLOT * gi, B * H * T * T - GROUP * SLOT)
+            return out_flat[base : base + GROUP * SLOT]
+
+        def park(gi):
             st = stg[gi % NSTG]
             nc.scalar.copy(
                 out=st[:].rearrange("p (i c) -> p i c", i=GROUP)[:, :, 1 : T + 1],
                 in_=rels[gi][:].rearrange("p (i j) -> p i j", i=GROUP),
             )
-            base = min(GROUP * SLOT * gi, B * H * T * T - GROUP * SLOT)
-            area = out_flat[base : base + GROUP * SLOT]
-            nc.sync.dma_start(
-                out=area.rearrange("(i t c) -> t i c", i=GROUP, t=T),
+            nc.scalar.dma_start(
+                out=area_of(gi).rearrange("(i t c) -> t i c", i=GROUP, t=T),
                 in_=st[:].rearrange("p (i c) -> p i c", i=GROUP),
             )
+
+        def fetch(gi):
             rb = back_pool.tile([P, GROUP * T], F32, tag="rb")
-            nc.sync.dma_start(
+            nc.scalar.dma_start(
                 out=rb[:].rearrange("p (i j) -> p i j", i=GROUP),
-                in_=area.rearrange("(i f) -> i f", i=GROUP)[:, T:SLOT].rearrange("i (t j) -> t i j", t=T),
+                in_=area_of(gi).rearrange("(i f) -> i f", i=GROUP)[:, T:SLOT].rearrange("i (t j) -> t i j", t=T),
             )
             rbs[gi] = rb
 
-        def back(gi):
-            cont = psum.tile([P, 512], F32, tag="cont")
-            for i in range(GROUP):
-                b = 2 * gi + i // 2
-                h = i % 2
-                for g in range(2):
-                    a = 128 * (2 * h + g)
-                    nc.tensor.matmul_mx(
-                        out=cont[:, 128 * i : 128 * i + 128],
-                        lhsT=qcs[b][:, a : a + 128].bitcast(FP8X4),
-                        lhsT_scale=qss[b][:, a : a + 128],
-                        rhs=kcs[b][:, a : a + 128].bitcast(FP8X4),
-                        rhs_scale=kss[b][:, a : a + 128],
-                        start=(g == 0),
-                        stop=(g == 1),
-                    )
+        def final_add(gi):
             fin = back_pool.tile([P, GROUP * T], F32, tag="fin")
-            nc.vector.tensor_tensor(out=fin[:], in0=cont[:], in1=rbs[gi][:], op=ADD)
-            nc.sync.dma_start(
+            nc.vector.tensor_tensor(out=fin[:], in0=conts[gi][:], in1=rbs[gi][:], op=ADD)
+            fins[gi] = fin
+
+        def final_store(gi):
+            nc.scalar.dma_start(
                 out=out[2 * gi : 2 * gi + 2].rearrange("b h t j -> t (b h) j"),
-                in_=fin[:].rearrange("p (i j) -> p i j", i=GROUP),
+                in_=fins[gi][:].rearrange("p (i j) -> p i j", i=GROUP),
             )
 
-        for gi in range(NGROUPS):
-            front(2 * gi)
-            front(2 * gi + 1)
-            shift_trip(gi)
-            if gi >= LAG:
-                back(gi - LAG)
-        for gi in range(NGROUPS - LAG, NGROUPS):
-            back(gi)
+        def group_at(x):
+            if x % 2 == 1 and 0 <= x < B:
+                return x // 2
+            return None
+
+        for s in range(-AHEAD, B + LAG + 2):
+            load_q(s + AHEAD + 2)
+            load_k(s + AHEAD + 2 - LAG)
+            mult_rel(s - 1)
+            mult_content(s - 1 - LAG)
+            gi = group_at(s - 1)
+            if gi is not None:
+                park(gi)
+            gi = group_at(s - 2)
+            if gi is not None:
+                fetch(gi)
+            gi = group_at(s - 2 - LAG)
+            if gi is not None:
+                final_store(gi)
+            turn_q(s + AHEAD)
+            if s == -AHEAD + 1:
+                prepare_r_tensor()
+            turn_k(s + AHEAD - LAG)
+            g_r = add_bias(s, 1)
+            g_w = add_bias(s - LAG, 0)
+            if s == 0:
+                nc.vector.quantize_mx(out=rc[:].bitcast(FP8X4), scales=rs[:], in_=gr[:])
+            quantise(s, "r", g_r)
+            if 0 <= s - LAG < B:
+                quantise(s - LAG, "k", gks[s - LAG])
+            quantise(s - LAG, "w", g_w)
+            gi = group_at(s - 1 - LAG)
+            if gi is not None:
+                final_add(gi)

@@ -14,12 +14,12 @@ B, T, H, D = 32, 128, 2, 1024
 P = 128
 FLOPS = 2 * 2 * B * H * T * T * D
 
-GROUP = 4
-NGROUPS = B * H // GROUP
+PAIR = 2
+GROUP = PAIR * H
+STEPS = B // PAIR
 SLOT = (T + 1) * T
-LAG = 3
-AHEAD = 2
-NSTG = 4
+NSTG = 3
+W = GROUP * D
 
 
 def transpose_head(nc, bank, words, ident):
@@ -42,13 +42,13 @@ def tile_relativepositionembedding_pa_t_kernel(tc, q, k, r_w_bias, r_r_bias, rel
     out_flat = out.rearrange("b h t j -> (b h t j)")
     with ExitStack() as ctx:
         const = ctx.enter_context(tc.tile_pool(name="const", bufs=1))
-        io = ctx.enter_context(tc.tile_pool(name="io", bufs=4))
-        rawp = ctx.enter_context(tc.tile_pool(name="rawp", bufs=LAG + AHEAD + 2))
-        gkp = ctx.enter_context(tc.tile_pool(name="gkp", bufs=AHEAD + 2))
+        io = ctx.enter_context(tc.tile_pool(name="io", bufs=3))
+        rawp = ctx.enter_context(tc.tile_pool(name="rawp", bufs=4))
+        gkp = ctx.enter_context(tc.tile_pool(name="gkp", bufs=3))
         work = ctx.enter_context(tc.tile_pool(name="work", bufs=2))
-        codes = ctx.enter_context(tc.tile_pool(name="codes", bufs=3))
-        back_pool = ctx.enter_context(tc.tile_pool(name="backp", bufs=4))
-        psum = ctx.enter_context(tc.psum_pool(name="psum", bufs=2))
+        codes = ctx.enter_context(tc.tile_pool(name="codes", bufs=2))
+        back_pool = ctx.enter_context(tc.tile_pool(name="backp", bufs=3))
+        psum = ctx.enter_context(tc.psum_pool(name="psum", bufs=1))
         ctx.enter_context(tc.manual_schedule())
 
         ident = const.tile([P, P], F32)
@@ -62,22 +62,27 @@ def tile_relativepositionembedding_pa_t_kernel(tc, q, k, r_w_bias, r_r_bias, rel
         qts = {}
         kts = {}
 
-        def load_q(b):
-            if 0 <= b < B:
-                qt = io.tile([P, H * D], BF16, tag="q")
-                nc.sync.dma_start(out=qt[:], in_=q[b].rearrange("t h d -> t (h d)"))
-                qts[b] = qt
+        def load(t, src, tag, keep, split):
+            if not 0 <= t < STEPS:
+                return
+            x = io.tile([P, W], BF16, tag=tag)
+            if split:
+                for i in range(PAIR):
+                    nc.sync.dma_start(
+                        out=x[:, H * D * i : H * D * (i + 1)], in_=src[PAIR * t + i].rearrange("t h d -> t (h d)")
+                    )
+            else:
+                nc.sync.dma_start(
+                    out=x[:].rearrange("p (b x) -> p b x", b=PAIR),
+                    in_=src[PAIR * t : PAIR * t + PAIR].rearrange("b t h d -> t b (h d)"),
+                )
+            keep[t] = x
 
-        def load_k(b):
-            if 0 <= b < B:
-                kt = io.tile([P, H * D], BF16, tag="k")
-                nc.sync.dma_start(out=kt[:], in_=k[b].rearrange("t h d -> t (h d)"))
-                kts[b] = kt
-
-        load_q(0)
-        load_q(1)
+        load(0, q, "q", qts, True)
         rsb = const.tile([P, H * D], BF16)
         nc.sync.dma_start(out=rsb[:], in_=rel_pos_emb.rearrange("j h d -> j (h d)"))
+        load(1, q, "q", qts, False)
+        load(0, k, "k", kts, False)
 
         stg = []
         for s in range(NSTG):
@@ -85,7 +90,7 @@ def tile_relativepositionembedding_pa_t_kernel(tc, q, k, r_w_bias, r_r_bias, rel
             nc.vector.memset(st[:], 0.0)
             stg.append(st)
 
-        pb = psum.tile([P, 512], F32, tag="xk")
+        pb = psum.tile([P, 512], F32, tag="xk", bufs=3)
         brow_w = brow[:].bitcast(F32)
         for c in range(4):
             nc.tensor.transpose(pb[:, 128 * c : 128 * c + 128], brow_w[:, 128 * c : 128 * c + 128], ident[:])
@@ -110,7 +115,7 @@ def tile_relativepositionembedding_pa_t_kernel(tc, q, k, r_w_bias, r_r_bias, rel
             gr_w = gr[:].bitcast(F32)
             rsb_w = rsb[:].bitcast(F32)
             for h in range(H):
-                xr = psum.tile([P, 512], F32, tag="xk")
+                xr = psum.tile([P, 512], F32, tag="xk", bufs=3)
                 transpose_head(nc, xr, rsb_w[:, 512 * h : 512 * h + 512], ident[:])
                 leave_bank(nc, gr_w[:, 512 * h : 512 * h + 512], xr)
 
@@ -122,144 +127,133 @@ def tile_relativepositionembedding_pa_t_kernel(tc, q, k, r_w_bias, r_r_bias, rel
         rbs = {}
         fins = {}
 
-        def turn_q(b):
-            if not 0 <= b < B:
-                return
-            words = qts[b][:].bitcast(F32)
-            raw = rawp.tile([P, H * 512], F32, tag="raw")
-            for h in range(H):
-                xq = psum.tile([P, 512], F32, tag="xq")
-                transpose_head(nc, xq, words[:, 512 * h : 512 * h + 512], ident[:])
-                leave_bank(nc, raw[:, 512 * h : 512 * h + 512], xq)
-            raws[b] = raw
+        def turn(t, src, tag, dst_words):
+            words = src[:].bitcast(F32)
+            for i in range(GROUP):
+                bank = psum.tile([P, 512], F32, tag=tag, bufs=3)
+                transpose_head(nc, bank, words[:, 512 * i : 512 * i + 512], ident[:])
+                leave_bank(nc, dst_words[:, 512 * i : 512 * i + 512], bank)
 
-        def turn_k(b):
-            if not 0 <= b < B:
-                return
-            words = kts[b][:].bitcast(F32)
-            gk = gkp.tile([P, H * D], BF16, tag="gk", align_bytes=64)
-            gk_w = gk[:].bitcast(F32)
-            for h in range(H):
-                xk = psum.tile([P, 512], F32, tag="xk")
-                transpose_head(nc, xk, words[:, 512 * h : 512 * h + 512], ident[:])
-                leave_bank(nc, gk_w[:, 512 * h : 512 * h + 512], xk)
-            gks[b] = gk
+        def turn_q(t):
+            if 0 <= t < STEPS:
+                raw = rawp.tile([P, GROUP * 512], F32, tag="raw")
+                turn(t, qts[t], "xq", raw)
+                raws[t] = raw
 
-        def add_bias(b, w):
-            if not 0 <= b < B:
+        def turn_k(t):
+            if 0 <= t < STEPS:
+                gk = gkp.tile([P, W], BF16, tag="gk", align_bytes=64)
+                turn(t, kts[t], "xk", gk[:].bitcast(F32))
+                gks[t] = gk
+
+        def add_bias(t, w):
+            if not 0 <= t < STEPS:
                 return None
-            g_ = work.tile([P, H * D], BF16, tag="g%d" % w, align_bytes=64)
+            g_ = work.tile([P, W], BF16, tag="g%d" % w, align_bytes=64)
             nc.vector.tensor_tensor(
-                out=g_[:], in0=raws[b][:].bitcast(BF16), in1=bfull[:, 2 * D * w : 2 * D * w + 2 * D], op=ADD
+                out=g_[:].rearrange("p (b x) -> p b x", b=PAIR),
+                in0=raws[t][:].bitcast(BF16).rearrange("p (b x) -> p b x", b=PAIR),
+                in1=bfull[:, H * D * w : H * D * (w + 1)].unsqueeze(1).to_broadcast([P, PAIR, H * D]),
+                op=ADD,
             )
             return g_
 
-        def quantise(b, kind, src):
+        def quantise(t, kind, src):
             if src is None:
                 return
-            c_ = codes.tile([P, 512], U32, tag="c" + kind, align_bytes=64)
-            s_ = codes.tile([P, 512], U8, tag="s" + kind, align_bytes=64)
+            c_ = codes.tile([P, W // 4], U32, tag="c" + kind, align_bytes=64)
+            s_ = codes.tile([P, W // 4], U8, tag="s" + kind, align_bytes=64)
             nc.vector.quantize_mx(out=c_[:].bitcast(FP8X4), scales=s_[:], in_=src[:])
-            cod[(kind, b)] = (c_, s_)
+            cod[(kind, t)] = (c_, s_)
 
-        def multiply(bank, b, left, right):
+        def multiply(bank, left, right, shared):
             lc, ls = left
             mc, ms = right
-            for h in range(H):
-                i = 2 * (b % 2) + h
+            for i in range(GROUP):
                 for g in range(2):
-                    a = 128 * (2 * h + g)
+                    a = 128 * (2 * i + g)
+                    m = 128 * (2 * (i % H) + g) if shared else a
                     nc.tensor.matmul_mx(
                         out=bank[:, 128 * i : 128 * i + 128],
                         lhsT=lc[:, a : a + 128].bitcast(FP8X4),
                         lhsT_scale=ls[:, a : a + 128],
-                        rhs=mc[:, a : a + 128].bitcast(FP8X4),
-                        rhs_scale=ms[:, a : a + 128],
+                        rhs=mc[:, m : m + 128].bitcast(FP8X4),
+                        rhs_scale=ms[:, m : m + 128],
                         start=(g == 0),
                         stop=(g == 1),
                     )
 
-        def mult_rel(b):
-            if not 0 <= b < B:
-                return
-            if b % 2 == 0:
-                rel_new = psum.tile([P, 512], F32, tag="rel")
-                rels[b // 2] = rel_new
-            multiply(rels[b // 2], b, cod[("r", b)], (rc, rs))
+        def mult_rel(t):
+            if 0 <= t < STEPS:
+                rel = psum.tile([P, 512], F32, tag="rel")
+                multiply(rel, cod[("r", t)], (rc, rs), True)
+                rels[t] = rel
 
-        def mult_content(b):
-            if not 0 <= b < B:
-                return
-            if b % 2 == 0:
-                cont_new = psum.tile([P, 512], F32, tag="cont")
-                conts[b // 2] = cont_new
-            multiply(conts[b // 2], b, cod[("w", b)], cod[("k", b)])
+        def mult_content(t):
+            if 0 <= t < STEPS:
+                cont = psum.tile([P, 512], F32, tag="cont")
+                multiply(cont, cod[("w", t)], cod[("k", t)], False)
+                conts[t] = cont
 
-        def area_of(gi):
-            base = min(GROUP * SLOT * gi, B * H * T * T - GROUP * SLOT)
+        def area_of(t):
+            base = min(GROUP * SLOT * t, B * H * T * T - GROUP * SLOT)
             return out_flat[base : base + GROUP * SLOT]
 
-        def park(gi):
-            st = stg[gi % NSTG]
-            nc.scalar.copy(
-                out=st[:].rearrange("p (i c) -> p i c", i=GROUP)[:, :, 1 : T + 1],
-                in_=rels[gi][:].rearrange("p (i j) -> p i j", i=GROUP),
-            )
-            nc.scalar.dma_start(
-                out=area_of(gi).rearrange("(i t c) -> t i c", i=GROUP, t=T),
-                in_=st[:].rearrange("p (i c) -> p i c", i=GROUP),
-            )
+        def pad_rel(t):
+            if 0 <= t < STEPS:
+                nc.scalar.copy(
+                    out=stg[t % NSTG][:].rearrange("p (i c) -> p i c", i=GROUP)[:, :, 1 : T + 1],
+                    in_=rels[t][:].rearrange("p (i j) -> p i j", i=GROUP),
+                )
 
-        def fetch(gi):
-            rb = back_pool.tile([P, GROUP * T], F32, tag="rb")
-            nc.scalar.dma_start(
-                out=rb[:].rearrange("p (i j) -> p i j", i=GROUP),
-                in_=area_of(gi).rearrange("(i f) -> i f", i=GROUP)[:, T:SLOT].rearrange("i (t j) -> t i j", t=T),
-            )
-            rbs[gi] = rb
+        def park(t):
+            if 0 <= t < STEPS:
+                nc.sync.dma_start(
+                    out=area_of(t).rearrange("(i t c) -> t i c", i=GROUP, t=T),
+                    in_=stg[t % NSTG][:].rearrange("p (i c) -> p i c", i=GROUP),
+                )
 
-        def final_add(gi):
-            fin = back_pool.tile([P, GROUP * T], F32, tag="fin")
-            nc.vector.tensor_tensor(out=fin[:], in0=conts[gi][:], in1=rbs[gi][:], op=ADD)
-            fins[gi] = fin
+        def fetch(t):
+            if 0 <= t < STEPS:
+                rb = back_pool.tile([P, GROUP * T], F32, tag="rb")
+                nc.sync.dma_start(
+                    out=rb[:].rearrange("p (i j) -> p i j", i=GROUP),
+                    in_=area_of(t).rearrange("(i f) -> i f", i=GROUP)[:, T:SLOT].rearrange("i (t j) -> t i j", t=T),
+                )
+                rbs[t] = rb
 
-        def final_store(gi):
-            nc.scalar.dma_start(
-                out=out[2 * gi : 2 * gi + 2].rearrange("b h t j -> t (b h) j"),
-                in_=fins[gi][:].rearrange("p (i j) -> p i j", i=GROUP),
-            )
+        def final_add(t):
+            if 0 <= t < STEPS:
+                fin = back_pool.tile([P, GROUP * T], F32, tag="fin")
+                nc.vector.tensor_tensor(out=fin[:], in0=conts[t][:], in1=rbs[t][:], op=ADD)
+                fins[t] = fin
 
-        def group_at(x):
-            if x % 2 == 1 and 0 <= x < B:
-                return x // 2
-            return None
+        def final_store(t):
+            if 0 <= t < STEPS:
+                nc.sync.dma_start(
+                    out=out[PAIR * t : PAIR * t + PAIR].rearrange("b h t j -> t (b h) j"),
+                    in_=fins[t][:].rearrange("p (i j) -> p i j", i=GROUP),
+                )
 
-        for s in range(-AHEAD, B + LAG + 2):
-            load_q(s + AHEAD + 2)
-            load_k(s + AHEAD + 2 - LAG)
-            mult_rel(s - 1)
-            mult_content(s - 1 - LAG)
-            gi = group_at(s - 1)
-            if gi is not None:
-                park(gi)
-            gi = group_at(s - 2)
-            if gi is not None:
-                fetch(gi)
-            gi = group_at(s - 2 - LAG)
-            if gi is not None:
-                final_store(gi)
-            turn_q(s + AHEAD)
-            if s == -AHEAD + 1:
+        for t in range(-1, STEPS + 2):
+            load(t + 3, q, "q", qts, False)
+            load(t + 2, k, "k", kts, False)
+            mult_content(t - 2)
+            turn_q(t + 1)
+            if t == -1:
                 prepare_r_tensor()
-            turn_k(s + AHEAD - LAG)
-            g_r = add_bias(s, 1)
-            g_w = add_bias(s - LAG, 0)
-            if s == 0:
+            g_r = add_bias(t, 1)
+            final_add(t - 2)
+            if t == 0:
                 nc.vector.quantize_mx(out=rc[:].bitcast(FP8X4), scales=rs[:], in_=gr[:])
-            quantise(s, "r", g_r)
-            if 0 <= s - LAG < B:
-                quantise(s - LAG, "k", gks[s - LAG])
-            quantise(s - LAG, "w", g_w)
-            gi = group_at(s - 1 - LAG)
-            if gi is not None:
-                final_add(gi)
+            quantise(t, "r", g_r)
+            mult_rel(t)
+            pad_rel(t)
+            turn_k(t)
+            g_w = add_bias(t - 1, 0)
+            if 0 <= t - 1 < STEPS:
+                quantise(t - 1, "k", gks[t - 1])
+            quantise(t - 1, "w", g_w)
+            fetch(t - 1)
+            final_store(t - 2)
+            park(t)

@@ -9,17 +9,34 @@ U32 = mybir.dt.uint32
 U8 = mybir.dt.uint8
 FP8X4 = mybir.dt.float8_e4m3fn_x4
 ADD = mybir.AluOpType.add
+IDENTITY = mybir.ActivationFunctionType.Identity
 
 B, T, H, D = 32, 128, 2, 1024
 P = 128
 FLOPS = 2 * 2 * B * H * T * T * D
 
-PAIR = 2
-GROUP = PAIR * H
-STEPS = B // PAIR
+GROUP = 4
+NGROUPS = B * H // GROUP
 SLOT = (T + 1) * T
 NSTG = 3
-W = GROUP * D
+
+NF = B - 4
+TAIL = 4
+PF = 3
+PERIOD = 4
+FIRST_SPECIAL = 7
+
+
+def is_special(b):
+    return FIRST_SPECIAL <= b < NF and b % PERIOD == FIRST_SPECIAL % PERIOD
+
+
+def c_step(b):
+    return b if b < NF else b + TAIL
+
+
+def fa_step(gi):
+    return {12: 30, 13: 34, 14: 35, 15: 37}.get(gi, 2 * gi + 5)
 
 
 def transpose_head(nc, bank, words, ident):
@@ -42,13 +59,12 @@ def tile_relativepositionembedding_pa_t_kernel(tc, q, k, r_w_bias, r_r_bias, rel
     out_flat = out.rearrange("b h t j -> (b h t j)")
     with ExitStack() as ctx:
         const = ctx.enter_context(tc.tile_pool(name="const", bufs=1))
-        io = ctx.enter_context(tc.tile_pool(name="io", bufs=3))
-        rawp = ctx.enter_context(tc.tile_pool(name="rawp", bufs=4))
-        gkp = ctx.enter_context(tc.tile_pool(name="gkp", bufs=3))
-        work = ctx.enter_context(tc.tile_pool(name="work", bufs=2))
-        codes = ctx.enter_context(tc.tile_pool(name="codes", bufs=2))
+        io = ctx.enter_context(tc.tile_pool(name="io", bufs=PF + 2))
+        rawp = ctx.enter_context(tc.tile_pool(name="rawp", bufs=TAIL + 1))
+        work = ctx.enter_context(tc.tile_pool(name="work", bufs=3))
+        codes = ctx.enter_context(tc.tile_pool(name="codes", bufs=7))
         back_pool = ctx.enter_context(tc.tile_pool(name="backp", bufs=3))
-        psum = ctx.enter_context(tc.psum_pool(name="psum", bufs=1))
+        psum = ctx.enter_context(tc.psum_pool(name="psum", bufs=2))
         ctx.enter_context(tc.manual_schedule())
 
         ident = const.tile([P, P], F32)
@@ -60,29 +76,37 @@ def tile_relativepositionembedding_pa_t_kernel(tc, q, k, r_w_bias, r_r_bias, rel
         nc.sync.dma_start(out=brow[2:4, :], in_=r_r_bias)
 
         qts = {}
+        qss = {}
         kts = {}
 
-        def load(t, src, tag, keep, split):
-            if not 0 <= t < STEPS:
-                return
-            x = io.tile([P, W], BF16, tag=tag)
-            if split:
-                for i in range(PAIR):
-                    nc.sync.dma_start(
-                        out=x[:, H * D * i : H * D * (i + 1)], in_=src[PAIR * t + i].rearrange("t h d -> t (h d)")
-                    )
-            else:
-                nc.sync.dma_start(
-                    out=x[:].rearrange("p (b x) -> p b x", b=PAIR),
-                    in_=src[PAIR * t : PAIR * t + PAIR].rearrange("b t h d -> t b (h d)"),
-                )
-            keep[t] = x
+        def load_q(b):
+            if 0 <= b < B:
+                qt = io.tile([P, H * D], BF16, tag="q")
+                if is_special(b):
+                    nc.sync.dma_start(out=qt[:, 0:D], in_=q[b][:, 0, :])
+                else:
+                    nc.sync.dma_start(out=qt[:], in_=q[b].rearrange("t h d -> t (h d)"))
+                qts[b] = qt
 
-        load(0, q, "q", qts, True)
+        def load_q_special(b):
+            if is_special(b):
+                qh = io.tile([P, D], BF16, tag="qh", bufs=2)
+                nc.sync.dma_start(out=qh[:], in_=q[b][:, 1, :])
+                qss[b] = qh
+
+        def load_k(b):
+            if 0 <= b < B:
+                kt = io.tile([P, H * D], BF16, tag="k")
+                nc.sync.dma_start(out=kt[:], in_=k[b].rearrange("t h d -> t (h d)"))
+                kts[b] = kt
+
+        load_q(0)
+        load_k(0)
         rsb = const.tile([P, H * D], BF16)
         nc.sync.dma_start(out=rsb[:], in_=rel_pos_emb.rearrange("j h d -> j (h d)"))
-        load(1, q, "q", qts, False)
-        load(0, k, "k", kts, False)
+        for b in range(1, PF):
+            load_q(b)
+            load_k(b)
 
         stg = []
         for s in range(NSTG):
@@ -90,7 +114,7 @@ def tile_relativepositionembedding_pa_t_kernel(tc, q, k, r_w_bias, r_r_bias, rel
             nc.vector.memset(st[:], 0.0)
             stg.append(st)
 
-        pb = psum.tile([P, 512], F32, tag="xk", bufs=3)
+        pb = psum.tile([P, 512], F32, tag="xk")
         brow_w = brow[:].bitcast(F32)
         for c in range(4):
             nc.tensor.transpose(pb[:, 128 * c : 128 * c + 128], brow_w[:, 128 * c : 128 * c + 128], ident[:])
@@ -101,11 +125,13 @@ def tile_relativepositionembedding_pa_t_kernel(tc, q, k, r_w_bias, r_r_bias, rel
         )
         bfull = const.tile([P, 4 * D], BF16, align_bytes=64)
         bfull_w = bfull[:].bitcast(F32)
-        for i in (2, 3, 0, 1):
+        for i in (2, 0, 3, 1):
             nc.vector.tensor_copy(
                 out=bfull_w[:, 512 * i : 512 * i + 512].rearrange("p (g r u) -> p g r u", g=2, u=2),
                 in_=bsm[:, 4 * i : 4 * i + 4].rearrange("p (g u) -> p g u", g=2).unsqueeze(2).to_broadcast([P, 2, T, 2]),
             )
+        b32 = const.tile([P, 32], F32)
+        nc.vector.tensor_copy(out=b32[:], in_=bsm[:].bitcast(BF16))
 
         gr = const.tile([P, H * D], BF16, align_bytes=64)
         rc = const.tile([P, 512], U32, align_bytes=64)
@@ -115,64 +141,119 @@ def tile_relativepositionembedding_pa_t_kernel(tc, q, k, r_w_bias, r_r_bias, rel
             gr_w = gr[:].bitcast(F32)
             rsb_w = rsb[:].bitcast(F32)
             for h in range(H):
-                xr = psum.tile([P, 512], F32, tag="xk", bufs=3)
+                xr = psum.tile([P, 512], F32, tag="xk")
                 transpose_head(nc, xr, rsb_w[:, 512 * h : 512 * h + 512], ident[:])
                 leave_bank(nc, gr_w[:, 512 * h : 512 * h + 512], xr)
 
+        xqs = {}
+        xss = {}
         raws = {}
         gks = {}
-        cod = {}
+        gts = {}
+        cod = {("e", 0): (rc, rs, 0)}
         rels = {}
         conts = {}
         rbs = {}
         fins = {}
 
-        def turn(t, src, tag, dst_words):
-            words = src[:].bitcast(F32)
-            for i in range(GROUP):
-                bank = psum.tile([P, 512], F32, tag=tag, bufs=3)
-                transpose_head(nc, bank, words[:, 512 * i : 512 * i + 512], ident[:])
-                leave_bank(nc, dst_words[:, 512 * i : 512 * i + 512], bank)
-
-        def turn_q(t):
-            if 0 <= t < STEPS:
-                raw = rawp.tile([P, GROUP * 512], F32, tag="raw")
-                turn(t, qts[t], "xq", raw)
-                raws[t] = raw
-
-        def turn_k(t):
-            if 0 <= t < STEPS:
-                gk = gkp.tile([P, W], BF16, tag="gk", align_bytes=64)
-                turn(t, kts[t], "xk", gk[:].bitcast(F32))
-                gks[t] = gk
-
-        def add_bias(t, w):
-            if not 0 <= t < STEPS:
-                return None
-            g_ = work.tile([P, W], BF16, tag="g%d" % w, align_bytes=64)
-            nc.vector.tensor_tensor(
-                out=g_[:].rearrange("p (b x) -> p b x", b=PAIR),
-                in0=raws[t][:].bitcast(BF16).rearrange("p (b x) -> p b x", b=PAIR),
-                in1=bfull[:, H * D * w : H * D * (w + 1)].unsqueeze(1).to_broadcast([P, PAIR, H * D]),
-                op=ADD,
-            )
-            return g_
-
-        def quantise(t, kind, src):
-            if src is None:
+        def turn_q(b):
+            if not 0 <= b < B:
                 return
-            c_ = codes.tile([P, W // 4], U32, tag="c" + kind, align_bytes=64)
-            s_ = codes.tile([P, W // 4], U8, tag="s" + kind, align_bytes=64)
-            nc.vector.quantize_mx(out=c_[:].bitcast(FP8X4), scales=s_[:], in_=src[:])
-            cod[(kind, t)] = (c_, s_)
+            words = qts[b][:].bitcast(F32)
+            if b >= NF:
+                raw = rawp.tile([P, H * 512], F32, tag="raw")
+                raws[b] = raw
+            for h in range(H):
+                if h == 1 and is_special(b):
+                    continue
+                xq = psum.tile([P, 512], F32, tag="xq")
+                transpose_head(nc, xq, words[:, 512 * h : 512 * h + 512], ident[:])
+                if b >= NF:
+                    leave_bank(nc, raws[b][:, 512 * h : 512 * h + 512], xq)
+                else:
+                    xqs[(b, h)] = xq
 
-        def multiply(bank, left, right, shared):
-            lc, ls = left
-            mc, ms = right
-            for i in range(GROUP):
+        def turn_special(b):
+            if is_special(b):
+                xs = psum.tile([P, 512], F32, tag="xs")
+                transpose_head(nc, xs, qss[b][:].bitcast(F32), ident[:])
+                xss[b] = xs
+                gs = work.tile([P, 4 * D], BF16, tag="gs", bufs=2, align_bytes=64)
+                gts[b] = gs
+
+        def turn_k(b):
+            words = kts[b][:].bitcast(F32)
+            gk = work.tile([P, H * D], BF16, tag="gk", align_bytes=64)
+            gk_w = gk[:].bitcast(F32)
+            for h in range(H):
+                xk = psum.tile([P, 512], F32, tag="xk")
+                transpose_head(nc, xk, words[:, 512 * h : 512 * h + 512], ident[:])
+                leave_bank(nc, gk_w[:, 512 * h : 512 * h + 512], xk)
+            gks[b] = gk
+
+        def sums(s):
+            if 0 <= s < NF:
+                if not is_special(s):
+                    g_new = work.tile([P, 4 * D], BF16, tag="g", align_bytes=64)
+                    gts[s] = g_new
+                for h in range(H):
+                    if h == 1 and is_special(s):
+                        continue
+                    bank = xqs[(s, h)][:].bitcast(BF16).rearrange("p (u x e) -> p x u e", u=2, e=2)
+                    for side in range(2):
+                        i = 2 * (1 - side) + h
+                        o = D * (2 * side + h)
+                        nc.vector.tensor_tensor(
+                            out=gts[s][:, o : o + D].rearrange("p (x u e) -> p x u e", u=2, e=2),
+                            in0=bank,
+                            in1=bfull[:, D * i : D * i + D].rearrange("p (x u e) -> p x u e", u=2, e=2),
+                            op=ADD,
+                        )
+            for side, b in ((0, s), (1, s - TAIL)):
+                if NF <= b < B:
+                    g_tail = work.tile([P, 4 * D], BF16, tag="g", align_bytes=64)
+                    i = 2 * (1 - side)
+                    nc.vector.tensor_tensor(
+                        out=g_tail[:, 0 : H * D], in0=raws[b][:].bitcast(BF16), in1=bfull[:, D * i : D * i + H * D], op=ADD
+                    )
+                    gts[(side, b)] = g_tail
+
+        def quantise_q(src, width):
+            cq = codes.tile([P, D], U32, tag="cq", align_bytes=64)
+            sq = codes.tile([P, D], U8, tag="sq", align_bytes=64)
+            nc.vector.quantize_mx(
+                out=cq[:, 0 : width // 4].bitcast(FP8X4), scales=sq[:, 0 : width // 4], in_=src[:, 0:width]
+            )
+            return cq, sq
+
+        def quantise_k(b):
+            ck = codes.tile([P, 512], U32, tag="ck", align_bytes=64)
+            sk = codes.tile([P, 512], U8, tag="sk", align_bytes=64)
+            nc.vector.quantize_mx(out=ck[:].bitcast(FP8X4), scales=sk[:], in_=gks[b][:])
+            cod[("k", b)] = (ck, sk, 0)
+
+        def quants(j):
+            if 0 <= j < NF:
+                cq, sq = quantise_q(gts[j], 4 * D)
+                cod[("r", j)] = (cq, sq, 0)
+                cod[("w", j)] = (cq, sq, 512)
+                quantise_k(j)
+            if NF <= j < B:
+                cq, sq = quantise_q(gts[(0, j)], H * D)
+                cod[("r", j)] = (cq, sq, 0)
+            if NF <= j - TAIL < B:
+                cq, sq = quantise_q(gts[(1, j - TAIL)], H * D)
+                cod[("w", j - TAIL)] = (cq, sq, 0)
+                quantise_k(j - TAIL)
+
+        def multiply(bank, b, left, right):
+            lc, ls, lb = left
+            mc, ms, mb = right
+            for h in range(H):
+                i = 2 * (b % 2) + h
                 for g in range(2):
-                    a = 128 * (2 * i + g)
-                    m = 128 * (2 * (i % H) + g) if shared else a
+                    a = lb + 128 * (2 * h + g)
+                    m = mb + 128 * (2 * h + g)
                     nc.tensor.matmul_mx(
                         out=bank[:, 128 * i : 128 * i + 128],
                         lhsT=lc[:, a : a + 128].bitcast(FP8X4),
@@ -183,77 +264,110 @@ def tile_relativepositionembedding_pa_t_kernel(tc, q, k, r_w_bias, r_r_bias, rel
                         stop=(g == 1),
                     )
 
-        def mult_rel(t):
-            if 0 <= t < STEPS:
-                rel = psum.tile([P, 512], F32, tag="rel")
-                multiply(rel, cod[("r", t)], (rc, rs), True)
-                rels[t] = rel
+        def mult_rel(b):
+            if 0 <= b < B:
+                if b % 2 == 0:
+                    rel_new = psum.tile([P, 512], F32, tag="rel", bufs=1)
+                    rels[b // 2] = rel_new
+                multiply(rels[b // 2], b, cod[("r", b)], cod[("e", 0)])
 
-        def mult_content(t):
-            if 0 <= t < STEPS:
-                cont = psum.tile([P, 512], F32, tag="cont")
-                multiply(cont, cod[("w", t)], cod[("k", t)], False)
-                conts[t] = cont
+        def mult_content(gi):
+            cont = psum.tile([P, 512], F32, tag="cont", bufs=1)
+            for b in (2 * gi, 2 * gi + 1):
+                multiply(cont, b, cod[("w", b)], cod[("k", b)])
+            conts[gi] = cont
 
-        def area_of(t):
-            base = min(GROUP * SLOT * t, B * H * T * T - GROUP * SLOT)
+        def offload(s):
+            for b in range(s + 1, s + PERIOD + 1):
+                if is_special(b):
+                    n = 16 // PERIOD
+                    first = n * (s - (b - PERIOD))
+                    bank = xss[b][:].bitcast(BF16).rearrange("p (c r e) -> p c r e", c=4, e=2)
+                    for idx in range(first, first + n):
+                        side = idx // 8
+                        g = (idx // 4) % 2
+                        u = (idx // 2) % 2
+                        e = idx % 2
+                        col = 8 * (2 * (1 - side) + 1) + 4 * g + 2 * u + e
+                        o = D * (2 * side + 1) + 512 * g
+                        nc.scalar.activation(
+                            out=gts[b][:, o : o + 512].rearrange("p (r j) -> p r j", j=4)[:, :, 2 * u + e],
+                            in_=bank[:, 2 * u + g, :, e],
+                            func=IDENTITY,
+                            bias=b32[:, col : col + 1],
+                            scale=1.0,
+                        )
+
+        def area_of(gi):
+            base = min(GROUP * SLOT * gi, B * H * T * T - GROUP * SLOT)
             return out_flat[base : base + GROUP * SLOT]
 
-        def pad_rel(t):
-            if 0 <= t < STEPS:
-                nc.scalar.copy(
-                    out=stg[t % NSTG][:].rearrange("p (i c) -> p i c", i=GROUP)[:, :, 1 : T + 1],
-                    in_=rels[t][:].rearrange("p (i j) -> p i j", i=GROUP),
-                )
+        def pad_rel(gi):
+            nc.scalar.copy(
+                out=stg[gi % NSTG][:].rearrange("p (i c) -> p i c", i=GROUP)[:, :, 1 : T + 1],
+                in_=rels[gi][:].rearrange("p (i j) -> p i j", i=GROUP),
+            )
 
-        def park(t):
-            if 0 <= t < STEPS:
-                nc.sync.dma_start(
-                    out=area_of(t).rearrange("(i t c) -> t i c", i=GROUP, t=T),
-                    in_=stg[t % NSTG][:].rearrange("p (i c) -> p i c", i=GROUP),
-                )
+        def park(gi):
+            nc.sync.dma_start(
+                out=area_of(gi).rearrange("(i t c) -> t i c", i=GROUP, t=T),
+                in_=stg[gi % NSTG][:].rearrange("p (i c) -> p i c", i=GROUP),
+            )
 
-        def fetch(t):
-            if 0 <= t < STEPS:
-                rb = back_pool.tile([P, GROUP * T], F32, tag="rb")
-                nc.sync.dma_start(
-                    out=rb[:].rearrange("p (i j) -> p i j", i=GROUP),
-                    in_=area_of(t).rearrange("(i f) -> i f", i=GROUP)[:, T:SLOT].rearrange("i (t j) -> t i j", t=T),
-                )
-                rbs[t] = rb
+        def fetch(gi):
+            rb = back_pool.tile([P, GROUP * T], F32, tag="rb")
+            nc.sync.dma_start(
+                out=rb[:].rearrange("p (i j) -> p i j", i=GROUP),
+                in_=area_of(gi).rearrange("(i f) -> i f", i=GROUP)[:, T:SLOT].rearrange("i (t j) -> t i j", t=T),
+            )
+            rbs[gi] = rb
 
-        def final_add(t):
-            if 0 <= t < STEPS:
-                fin = back_pool.tile([P, GROUP * T], F32, tag="fin")
-                nc.vector.tensor_tensor(out=fin[:], in0=conts[t][:], in1=rbs[t][:], op=ADD)
-                fins[t] = fin
+        def final_add(gi):
+            fin = back_pool.tile([P, GROUP * T], F32, tag="fin")
+            nc.vector.tensor_tensor(out=fin[:], in0=conts[gi][:], in1=rbs[gi][:], op=ADD)
+            fins[gi] = fin
 
-        def final_store(t):
-            if 0 <= t < STEPS:
-                nc.sync.dma_start(
-                    out=out[PAIR * t : PAIR * t + PAIR].rearrange("b h t j -> t (b h) j"),
-                    in_=fins[t][:].rearrange("p (i j) -> p i j", i=GROUP),
-                )
+        def final_store(gi):
+            nc.sync.dma_start(
+                out=out[2 * gi : 2 * gi + 2].rearrange("b h t j -> t (b h) j"),
+                in_=fins[gi][:].rearrange("p (i j) -> p i j", i=GROUP),
+            )
 
-        for t in range(-1, STEPS + 2):
-            load(t + 3, q, "q", qts, False)
-            load(t + 2, k, "k", kts, False)
-            mult_content(t - 2)
-            turn_q(t + 1)
-            if t == -1:
+        groups = range(NGROUPS)
+        for s in range(-1, fa_step(NGROUPS - 1) + 1):
+            load_q(s + 1 + PF)
+            for b in range(PF, B):
+                if c_step(b) == s + 1 + PF:
+                    load_k(b)
+            load_q_special(s + PERIOD + PF)
+            due = [gi for gi in groups if fa_step(gi) == s]
+            padded = [gi for gi in groups if 2 * gi + 3 == s]
+            for gi in due:
+                mult_content(gi)
+            for gi in padded:
+                pad_rel(gi)
+            next_k = [b for b in range(B) if c_step(b) == s + 1]
+            if s >= 0:
+                for b in next_k:
+                    turn_k(b)
+            turn_special(s + PERIOD)
+            sums(s)
+            turn_q(s + 1)
+            if s == -1:
+                for b in next_k:
+                    turn_k(b)
                 prepare_r_tensor()
-            g_r = add_bias(t, 1)
-            final_add(t - 2)
-            if t == 0:
+            if s == 1:
                 nc.vector.quantize_mx(out=rc[:].bitcast(FP8X4), scales=rs[:], in_=gr[:])
-            quantise(t, "r", g_r)
-            mult_rel(t)
-            pad_rel(t)
-            turn_k(t)
-            g_w = add_bias(t - 1, 0)
-            if 0 <= t - 1 < STEPS:
-                quantise(t - 1, "k", gks[t - 1])
-            quantise(t - 1, "w", g_w)
-            fetch(t - 1)
-            final_store(t - 2)
-            park(t)
+            quants(s - 1)
+            mult_rel(s - 1)
+            offload(s)
+            for gi in due:
+                final_add(gi)
+            for gi in groups:
+                if 2 * gi + 4 == s:
+                    fetch(gi)
+            for gi in padded:
+                park(gi)
+            for gi in due:
+                final_store(gi)

@@ -23,8 +23,8 @@ NSTG = 3
 NF = B - 4
 TAIL = 4
 PF = 3
-PERIOD = 4
-FIRST_SPECIAL = 7
+PERIOD = 3
+FIRST_SPECIAL = PERIOD + PF
 
 
 def is_special(b):
@@ -280,10 +280,9 @@ def tile_relativepositionembedding_pa_t_kernel(tc, q, k, r_w_bias, r_r_bias, rel
         def offload(s):
             for b in range(s + 1, s + PERIOD + 1):
                 if is_special(b):
-                    n = 16 // PERIOD
-                    first = n * (s - (b - PERIOD))
+                    part = s - (b - PERIOD)
                     bank = xss[b][:].bitcast(BF16).rearrange("p (c r e) -> p c r e", c=4, e=2)
-                    for idx in range(first, first + n):
+                    for idx in range(16 * part // PERIOD, 16 * (part + 1) // PERIOD):
                         side = idx // 8
                         g = (idx // 4) % 2
                         u = (idx // 2) % 2

@@ -15,43 +15,73 @@ B, T, H, D = 32, 128, 2, 1024
 P = 128
 FLOPS = 2 * 2 * B * H * T * T * D
 
+WORDS = D // 2
+CODES = D // 4
 GROUP = 4
 NGROUPS = B * H // GROUP
-SLOT = (T + 1) * T
-NSTG = 3
+PADDED = (T + 1) * T
 
-NF = B - 4
-TAIL = 4
-PF = 3
-PERIOD = 3
-FIRST_SPECIAL = PERIOD + PF
-
-
-def is_special(b):
-    return FIRST_SPECIAL <= b < NF and b % PERIOD == FIRST_SPECIAL % PERIOD
+PREFETCH = 3
+LATE = 4
+EARLY = B - LATE
+SCALAR_PERIOD = 3
+SCALAR_ADDS = 16
+FIRST_SCALAR_BATCH = SCALAR_PERIOD + PREFETCH
 
 
-def c_step(b):
-    return b if b < NF else b + TAIL
+def made_by_scalar(b):
+    return FIRST_SCALAR_BATCH <= b < EARLY and b % SCALAR_PERIOD == FIRST_SCALAR_BATCH % SCALAR_PERIOD
 
 
-def fa_step(gi):
-    return {12: 30, 13: 34, 14: 35, 15: 37}.get(gi, 2 * gi + 5)
+def w_step(b):
+    return b if b < EARLY else b + LATE
 
 
-def transpose_head(nc, bank, words, ident):
+def pad_step(gi):
+    return 2 * gi + 3
+
+
+def final_step(gi):
+    s = pad_step(gi)
+    halves = 2 if s < EARLY else 1
+    while halves < 5:
+        s += 1
+        halves += 2 if s < EARLY else 1
+    return max(s, w_step(2 * gi + 1) + 2)
+
+
+def transpose_matrix(nc, bank, words, identity):
     for u in range(2):
         for g in range(2):
-            c = 2 * u + g
-            src = 256 * g + 128 * u
-            nc.tensor.transpose(bank[:, 128 * c : 128 * c + 128], words[:, src : src + 128], ident)
+            block = 2 * u + g
+            first = 256 * g + 128 * u
+            nc.tensor.transpose(bank[:, P * block : P * block + P], words[:, first : first + P], identity)
 
 
-def leave_bank(nc, dst_words, bank):
+def copy_regrouped(nc, dst_words, bank):
     nc.scalar.copy(
         out=dst_words.rearrange("p (x u) -> p x u", u=2),
         in_=bank[:].rearrange("p (u x) -> p x u", u=2),
     )
+
+
+def multiply_batch(nc, bank, b, left, right):
+    left_codes, left_scales, left_first = left
+    right_codes, right_scales, right_first = right
+    for h in range(H):
+        matrix = H * (b % 2) + h
+        for g in range(2):
+            lo = left_first + P * (2 * h + g)
+            ro = right_first + P * (2 * h + g)
+            nc.tensor.matmul_mx(
+                out=bank[:, T * matrix : T * matrix + T],
+                lhsT=left_codes[:, lo : lo + P].bitcast(FP8X4),
+                lhsT_scale=left_scales[:, lo : lo + P],
+                rhs=right_codes[:, ro : ro + P].bitcast(FP8X4),
+                rhs_scale=right_scales[:, ro : ro + P],
+                start=(g == 0),
+                stop=(g == 1),
+            )
 
 
 def tile_relativepositionembedding_pa_t_kernel(tc, q, k, r_w_bias, r_r_bias, rel_pos_emb, out):
@@ -59,314 +89,306 @@ def tile_relativepositionembedding_pa_t_kernel(tc, q, k, r_w_bias, r_r_bias, rel
     out_flat = out.rearrange("b h t j -> (b h t j)")
     with ExitStack() as ctx:
         const = ctx.enter_context(tc.tile_pool(name="const", bufs=1))
-        io = ctx.enter_context(tc.tile_pool(name="io", bufs=PF + 2))
-        rawp = ctx.enter_context(tc.tile_pool(name="rawp", bufs=TAIL + 1))
-        work = ctx.enter_context(tc.tile_pool(name="work", bufs=3))
+        loads = ctx.enter_context(tc.tile_pool(name="loads", bufs=PREFETCH + 2))
+        kept = ctx.enter_context(tc.tile_pool(name="kept", bufs=LATE + 1))
+        sums_pool = ctx.enter_context(tc.tile_pool(name="sums", bufs=3))
         codes = ctx.enter_context(tc.tile_pool(name="codes", bufs=7))
-        back_pool = ctx.enter_context(tc.tile_pool(name="backp", bufs=3))
+        results = ctx.enter_context(tc.tile_pool(name="results", bufs=3))
         psum = ctx.enter_context(tc.psum_pool(name="psum", bufs=2))
         ctx.enter_context(tc.manual_schedule())
 
-        ident = const.tile([P, P], F32)
-        make_identity(nc, ident[:])
+        identity = const.tile([P, P], F32)
+        make_identity(nc, identity[:])
 
-        brow = const.tile([P, D], BF16)
-        nc.vector.memset(brow[:], 0.0)
-        nc.sync.dma_start(out=brow[0:2, :], in_=r_w_bias)
-        nc.sync.dma_start(out=brow[2:4, :], in_=r_r_bias)
+        bias_rows = const.tile([P, D], BF16)
+        nc.vector.memset(bias_rows[:], 0.0)
+        nc.sync.dma_start(out=bias_rows[0:H, :], in_=r_w_bias)
+        nc.sync.dma_start(out=bias_rows[H : 2 * H, :], in_=r_r_bias)
 
-        qts = {}
-        qss = {}
-        kts = {}
+        q_tiles = {}
+        q_head1_tiles = {}
+        k_tiles = {}
 
         def load_q(b):
-            if 0 <= b < B:
-                qt = io.tile([P, H * D], BF16, tag="q")
-                if is_special(b):
-                    nc.sync.dma_start(out=qt[:, 0:D], in_=q[b][:, 0, :])
-                else:
-                    nc.sync.dma_start(out=qt[:], in_=q[b].rearrange("t h d -> t (h d)"))
-                qts[b] = qt
+            if not 0 <= b < B:
+                return
+            q_tile = loads.tile([P, H * D], BF16, tag="q")
+            if made_by_scalar(b):
+                nc.sync.dma_start(out=q_tile[:, 0:D], in_=q[b][:, 0, :])
+            elif b == 0:
+                for h in range(H):
+                    nc.sync.dma_start(out=q_tile[:, D * h : D * h + D], in_=q[b][:, h, :])
+            else:
+                nc.sync.dma_start(out=q_tile[:], in_=q[b].rearrange("t h d -> t (h d)"))
+            q_tiles[b] = q_tile
 
-        def load_q_special(b):
-            if is_special(b):
-                qh = io.tile([P, D], BF16, tag="qh", bufs=2)
-                nc.sync.dma_start(out=qh[:], in_=q[b][:, 1, :])
-                qss[b] = qh
+        def load_q_head1(b):
+            if made_by_scalar(b):
+                q_head1 = loads.tile([P, D], BF16, tag="q_head1", bufs=2)
+                nc.sync.dma_start(out=q_head1[:], in_=q[b][:, 1, :])
+                q_head1_tiles[b] = q_head1
 
         def load_k(b):
-            if 0 <= b < B:
-                kt = io.tile([P, H * D], BF16, tag="k")
-                nc.sync.dma_start(out=kt[:], in_=k[b].rearrange("t h d -> t (h d)"))
-                kts[b] = kt
+            k_tile = loads.tile([P, H * D], BF16, tag="k")
+            nc.sync.dma_start(out=k_tile[:], in_=k[b].rearrange("t h d -> t (h d)"))
+            k_tiles[b] = k_tile
 
         load_q(0)
         load_k(0)
-        rsb = const.tile([P, H * D], BF16)
-        nc.sync.dma_start(out=rsb[:], in_=rel_pos_emb.rearrange("j h d -> j (h d)"))
-        for b in range(1, PF):
+        emb_rows = const.tile([P, H * D], BF16)
+        nc.sync.dma_start(out=emb_rows[:], in_=rel_pos_emb.rearrange("j h d -> j (h d)"))
+        for b in range(1, PREFETCH):
             load_q(b)
             load_k(b)
 
-        stg = []
-        for s in range(NSTG):
-            st = const.tile([P, GROUP * (T + 1)], F32, name="stg%d" % s)
-            nc.vector.memset(st[:], 0.0)
-            stg.append(st)
+        padded_tiles = []
+        for n in range(3):
+            padded = const.tile([P, GROUP * (T + 1)], F32, name="padded%d" % n)
+            nc.vector.memset(padded[:], 0.0)
+            padded_tiles.append(padded)
 
-        pb = psum.tile([P, 512], F32, tag="xk")
-        brow_w = brow[:].bitcast(F32)
+        bias_bank = psum.tile([P, WORDS], F32, tag="k_bank")
+        bias_words = bias_rows[:].bitcast(F32)
         for c in range(4):
-            nc.tensor.transpose(pb[:, 128 * c : 128 * c + 128], brow_w[:, 128 * c : 128 * c + 128], ident[:])
-        bsm = const.tile([P, 16], F32)
+            nc.tensor.transpose(bias_bank[:, P * c : P * c + P], bias_words[:, P * c : P * c + P], identity[:])
+        bias_small = const.tile([P, 16], F32)
         nc.vector.tensor_copy(
-            out=bsm[:].rearrange("p (i c) -> p i c", c=4),
-            in_=pb[:].rearrange("p (c i) -> p i c", c=4)[:, 0:4, :],
+            out=bias_small[:].rearrange("p (i c) -> p i c", c=4),
+            in_=bias_bank[:].rearrange("p (c i) -> p i c", c=4)[:, 0:4, :],
         )
-        bfull = const.tile([P, 4 * D], BF16, align_bytes=64)
-        bfull_w = bfull[:].bitcast(F32)
+        bias_wide = const.tile([P, 4 * D], BF16, align_bytes=64)
+        bias_wide_words = bias_wide[:].bitcast(F32)
         for i in (2, 0, 3, 1):
             nc.vector.tensor_copy(
-                out=bfull_w[:, 512 * i : 512 * i + 512].rearrange("p (g r u) -> p g r u", g=2, u=2),
-                in_=bsm[:, 4 * i : 4 * i + 4].rearrange("p (g u) -> p g u", g=2).unsqueeze(2).to_broadcast([P, 2, T, 2]),
+                out=bias_wide_words[:, WORDS * i : WORDS * i + WORDS].rearrange("p (g r u) -> p g r u", g=2, u=2),
+                in_=bias_small[:, 4 * i : 4 * i + 4]
+                .rearrange("p (g u) -> p g u", g=2)
+                .unsqueeze(2)
+                .to_broadcast([P, 2, T, 2]),
             )
-        b32 = const.tile([P, 32], F32)
-        nc.vector.tensor_copy(out=b32[:], in_=bsm[:].bitcast(BF16))
+        bias_f32 = const.tile([P, 32], F32)
+        nc.vector.tensor_copy(out=bias_f32[:], in_=bias_small[:].bitcast(BF16))
 
-        gr = const.tile([P, H * D], BF16, align_bytes=64)
-        rc = const.tile([P, 512], U32, align_bytes=64)
-        rs = const.tile([P, 512], U8, align_bytes=64)
+        emb_grouped = const.tile([P, H * D], BF16, align_bytes=64)
+        emb_codes = const.tile([P, H * CODES], U32, align_bytes=64)
+        emb_scales = const.tile([P, H * CODES], U8, align_bytes=64)
 
-        def prepare_r_tensor():
-            gr_w = gr[:].bitcast(F32)
-            rsb_w = rsb[:].bitcast(F32)
+        def transpose_emb():
             for h in range(H):
-                xr = psum.tile([P, 512], F32, tag="xk")
-                transpose_head(nc, xr, rsb_w[:, 512 * h : 512 * h + 512], ident[:])
-                leave_bank(nc, gr_w[:, 512 * h : 512 * h + 512], xr)
+                bank = psum.tile([P, WORDS], F32, tag="k_bank")
+                transpose_matrix(nc, bank, emb_rows[:].bitcast(F32)[:, WORDS * h : WORDS * h + WORDS], identity[:])
+                copy_regrouped(nc, emb_grouped[:].bitcast(F32)[:, WORDS * h : WORDS * h + WORDS], bank)
 
-        xqs = {}
-        xss = {}
-        raws = {}
-        gks = {}
-        gts = {}
-        cod = {("e", 0): (rc, rs, 0)}
-        rels = {}
-        conts = {}
-        rbs = {}
-        fins = {}
+        q_banks = {}
+        scalar_banks = {}
+        kept_q = {}
+        k_grouped = {}
+        sum_tiles = {}
+        code_of = {}
+        rel_banks = {}
+        content_banks = {}
+        shifted = {}
+        finished = {}
 
-        def turn_q(b):
-            if not 0 <= b < B:
+        def transpose_q(b, h):
+            if not 0 <= b < B or (h == 1 and made_by_scalar(b)):
                 return
-            words = qts[b][:].bitcast(F32)
-            if b >= NF:
-                raw = rawp.tile([P, H * 512], F32, tag="raw")
-                raws[b] = raw
+            bank = psum.tile([P, WORDS], F32, tag="q_bank")
+            transpose_matrix(nc, bank, q_tiles[b][:].bitcast(F32)[:, WORDS * h : WORDS * h + WORDS], identity[:])
+            if b < EARLY:
+                q_banks[(b, h)] = bank
+                return
+            if h == 0:
+                kept_tile = kept.tile([P, H * WORDS], F32, tag="kept_q")
+                kept_q[b] = kept_tile
+            copy_regrouped(nc, kept_q[b][:, WORDS * h : WORDS * h + WORDS], bank)
+
+        def transpose_q_for_scalar(b):
+            if made_by_scalar(b):
+                bank = psum.tile([P, WORDS], F32, tag="scalar_bank")
+                transpose_matrix(nc, bank, q_head1_tiles[b][:].bitcast(F32), identity[:])
+                scalar_banks[b] = bank
+                early_sums = sums_pool.tile([P, 4 * D], BF16, tag="sums_scalar", bufs=2, align_bytes=64)
+                sum_tiles[b] = early_sums
+
+        def transpose_k(b):
+            grouped = sums_pool.tile([P, H * D], BF16, tag="k_grouped", align_bytes=64)
             for h in range(H):
-                if h == 1 and is_special(b):
-                    continue
-                xq = psum.tile([P, 512], F32, tag="xq")
-                transpose_head(nc, xq, words[:, 512 * h : 512 * h + 512], ident[:])
-                if b >= NF:
-                    leave_bank(nc, raws[b][:, 512 * h : 512 * h + 512], xq)
-                else:
-                    xqs[(b, h)] = xq
+                bank = psum.tile([P, WORDS], F32, tag="k_bank")
+                transpose_matrix(nc, bank, k_tiles[b][:].bitcast(F32)[:, WORDS * h : WORDS * h + WORDS], identity[:])
+                copy_regrouped(nc, grouped[:].bitcast(F32)[:, WORDS * h : WORDS * h + WORDS], bank)
+            k_grouped[b] = grouped
 
-        def turn_special(b):
-            if is_special(b):
-                xs = psum.tile([P, 512], F32, tag="xs")
-                transpose_head(nc, xs, qss[b][:].bitcast(F32), ident[:])
-                xss[b] = xs
-                gs = work.tile([P, 4 * D], BF16, tag="gs", bufs=2, align_bytes=64)
-                gts[b] = gs
+        def bias_row(bias, h):
+            return H * (1 - bias) + h
 
-        def turn_k(b):
-            words = kts[b][:].bitcast(F32)
-            gk = work.tile([P, H * D], BF16, tag="gk", align_bytes=64)
-            gk_w = gk[:].bitcast(F32)
-            for h in range(H):
-                xk = psum.tile([P, 512], F32, tag="xk")
-                transpose_head(nc, xk, words[:, 512 * h : 512 * h + 512], ident[:])
-                leave_bank(nc, gk_w[:, 512 * h : 512 * h + 512], xk)
-            gks[b] = gk
-
-        def sums(s):
-            if 0 <= s < NF:
-                if not is_special(s):
-                    g_new = work.tile([P, 4 * D], BF16, tag="g", align_bytes=64)
-                    gts[s] = g_new
+        def add_biases(s):
+            if 0 <= s < EARLY:
+                if not made_by_scalar(s):
+                    both_sums = sums_pool.tile([P, 4 * D], BF16, tag="sums", align_bytes=64)
+                    sum_tiles[s] = both_sums
                 for h in range(H):
-                    if h == 1 and is_special(s):
+                    if h == 1 and made_by_scalar(s):
                         continue
-                    bank = xqs[(s, h)][:].bitcast(BF16).rearrange("p (u x e) -> p x u e", u=2, e=2)
-                    for side in range(2):
-                        i = 2 * (1 - side) + h
-                        o = D * (2 * side + h)
+                    bank = q_banks[(s, h)][:].bitcast(BF16).rearrange("p (u x e) -> p x u e", u=2, e=2)
+                    for bias in range(2):
+                        at = D * (H * bias + h)
+                        row = D * bias_row(bias, h)
                         nc.vector.tensor_tensor(
-                            out=gts[s][:, o : o + D].rearrange("p (x u e) -> p x u e", u=2, e=2),
+                            out=sum_tiles[s][:, at : at + D].rearrange("p (x u e) -> p x u e", u=2, e=2),
                             in0=bank,
-                            in1=bfull[:, D * i : D * i + D].rearrange("p (x u e) -> p x u e", u=2, e=2),
+                            in1=bias_wide[:, row : row + D].rearrange("p (x u e) -> p x u e", u=2, e=2),
                             op=ADD,
                         )
-            for side, b in ((0, s), (1, s - TAIL)):
-                if NF <= b < B:
-                    g_tail = work.tile([P, 4 * D], BF16, tag="g", align_bytes=64)
-                    i = 2 * (1 - side)
+            for bias, b in ((0, s), (1, s - LATE)):
+                if EARLY <= b < B:
+                    one_sum = sums_pool.tile([P, 4 * D], BF16, tag="sums", align_bytes=64)
+                    row = D * bias_row(bias, 0)
                     nc.vector.tensor_tensor(
-                        out=g_tail[:, 0 : H * D], in0=raws[b][:].bitcast(BF16), in1=bfull[:, D * i : D * i + H * D], op=ADD
+                        out=one_sum[:, 0 : H * D],
+                        in0=kept_q[b][:].bitcast(BF16),
+                        in1=bias_wide[:, row : row + H * D],
+                        op=ADD,
                     )
-                    gts[(side, b)] = g_tail
+                    sum_tiles[(bias, b)] = one_sum
 
-        def quantise_q(src, width):
-            cq = codes.tile([P, D], U32, tag="cq", align_bytes=64)
-            sq = codes.tile([P, D], U8, tag="sq", align_bytes=64)
+        def scalar_adds(s):
+            for b in range(s + 1, s + SCALAR_PERIOD + 1):
+                if not made_by_scalar(b):
+                    continue
+                part = s - (b - SCALAR_PERIOD)
+                bank = scalar_banks[b][:].bitcast(BF16).rearrange("p (c r e) -> p c r e", c=4, e=2)
+                for n in range(SCALAR_ADDS * part // SCALAR_PERIOD, SCALAR_ADDS * (part + 1) // SCALAR_PERIOD):
+                    bias, g, u, e = n // 8, n // 4 % 2, n // 2 % 2, n % 2
+                    at = D * (H * bias + 1) + 512 * g
+                    column = 8 * bias_row(bias, 1) + 4 * g + 2 * u + e
+                    nc.scalar.activation(
+                        out=sum_tiles[b][:, at : at + 512].rearrange("p (r j) -> p r j", j=4)[:, :, 2 * u + e],
+                        in_=bank[:, 2 * u + g, :, e],
+                        func=IDENTITY,
+                        bias=bias_f32[:, column : column + 1],
+                        scale=1.0,
+                    )
+
+        def quantise_sums(src, width):
+            packed = codes.tile([P, 4 * CODES], U32, tag="q_codes", align_bytes=64)
+            scales = codes.tile([P, 4 * CODES], U8, tag="q_scales", align_bytes=64)
             nc.vector.quantize_mx(
-                out=cq[:, 0 : width // 4].bitcast(FP8X4), scales=sq[:, 0 : width // 4], in_=src[:, 0:width]
+                out=packed[:, 0 : width // 4].bitcast(FP8X4), scales=scales[:, 0 : width // 4], in_=src[:, 0:width]
             )
-            return cq, sq
+            return packed, scales
 
         def quantise_k(b):
-            ck = codes.tile([P, 512], U32, tag="ck", align_bytes=64)
-            sk = codes.tile([P, 512], U8, tag="sk", align_bytes=64)
-            nc.vector.quantize_mx(out=ck[:].bitcast(FP8X4), scales=sk[:], in_=gks[b][:])
-            cod[("k", b)] = (ck, sk, 0)
+            packed = codes.tile([P, H * CODES], U32, tag="k_codes", align_bytes=64)
+            scales = codes.tile([P, H * CODES], U8, tag="k_scales", align_bytes=64)
+            nc.vector.quantize_mx(out=packed[:].bitcast(FP8X4), scales=scales[:], in_=k_grouped[b][:])
+            code_of[("k", b)] = (packed, scales, 0)
 
-        def quants(j):
-            if 0 <= j < NF:
-                cq, sq = quantise_q(gts[j], 4 * D)
-                cod[("r", j)] = (cq, sq, 0)
-                cod[("w", j)] = (cq, sq, 512)
-                quantise_k(j)
-            if NF <= j < B:
-                cq, sq = quantise_q(gts[(0, j)], H * D)
-                cod[("r", j)] = (cq, sq, 0)
-            if NF <= j - TAIL < B:
-                cq, sq = quantise_q(gts[(1, j - TAIL)], H * D)
-                cod[("w", j - TAIL)] = (cq, sq, 0)
-                quantise_k(j - TAIL)
+        def quantise_step(s):
+            if 0 <= s < EARLY:
+                packed, scales = quantise_sums(sum_tiles[s], 4 * D)
+                code_of[("q+r_r", s)] = (packed, scales, 0)
+                code_of[("q+r_w", s)] = (packed, scales, H * CODES)
+                quantise_k(s)
+            if EARLY <= s < B:
+                packed, scales = quantise_sums(sum_tiles[(0, s)], H * D)
+                code_of[("q+r_r", s)] = (packed, scales, 0)
+            if EARLY <= s - LATE < B:
+                packed, scales = quantise_sums(sum_tiles[(1, s - LATE)], H * D)
+                code_of[("q+r_w", s - LATE)] = (packed, scales, 0)
+                quantise_k(s - LATE)
 
-        def multiply(bank, b, left, right):
-            lc, ls, lb = left
-            mc, ms, mb = right
-            for h in range(H):
-                i = 2 * (b % 2) + h
-                for g in range(2):
-                    a = lb + 128 * (2 * h + g)
-                    m = mb + 128 * (2 * h + g)
-                    nc.tensor.matmul_mx(
-                        out=bank[:, 128 * i : 128 * i + 128],
-                        lhsT=lc[:, a : a + 128].bitcast(FP8X4),
-                        lhsT_scale=ls[:, a : a + 128],
-                        rhs=mc[:, m : m + 128].bitcast(FP8X4),
-                        rhs_scale=ms[:, m : m + 128],
-                        start=(g == 0),
-                        stop=(g == 1),
-                    )
-
-        def mult_rel(b):
+        def multiply_rel(b):
             if 0 <= b < B:
                 if b % 2 == 0:
-                    rel_new = psum.tile([P, 512], F32, tag="rel", bufs=1)
-                    rels[b // 2] = rel_new
-                multiply(rels[b // 2], b, cod[("r", b)], cod[("e", 0)])
+                    rel_bank = psum.tile([P, GROUP * T], F32, tag="rel", bufs=1)
+                    rel_banks[b // 2] = rel_bank
+                multiply_batch(nc, rel_banks[b // 2], b, code_of[("q+r_r", b)], (emb_codes, emb_scales, 0))
 
-        def mult_content(gi):
-            cont = psum.tile([P, 512], F32, tag="cont", bufs=1)
+        def multiply_content(gi):
+            content_bank = psum.tile([P, GROUP * T], F32, tag="content", bufs=1)
             for b in (2 * gi, 2 * gi + 1):
-                multiply(cont, b, cod[("w", b)], cod[("k", b)])
-            conts[gi] = cont
+                multiply_batch(nc, content_bank, b, code_of[("q+r_w", b)], code_of[("k", b)])
+            content_banks[gi] = content_bank
 
-        def offload(s):
-            for b in range(s + 1, s + PERIOD + 1):
-                if is_special(b):
-                    part = s - (b - PERIOD)
-                    bank = xss[b][:].bitcast(BF16).rearrange("p (c r e) -> p c r e", c=4, e=2)
-                    for idx in range(16 * part // PERIOD, 16 * (part + 1) // PERIOD):
-                        side = idx // 8
-                        g = (idx // 4) % 2
-                        u = (idx // 2) % 2
-                        e = idx % 2
-                        col = 8 * (2 * (1 - side) + 1) + 4 * g + 2 * u + e
-                        o = D * (2 * side + 1) + 512 * g
-                        nc.scalar.activation(
-                            out=gts[b][:, o : o + 512].rearrange("p (r j) -> p r j", j=4)[:, :, 2 * u + e],
-                            in_=bank[:, 2 * u + g, :, e],
-                            func=IDENTITY,
-                            bias=b32[:, col : col + 1],
-                            scale=1.0,
-                        )
-
-        def area_of(gi):
-            base = min(GROUP * SLOT * gi, B * H * T * T - GROUP * SLOT)
-            return out_flat[base : base + GROUP * SLOT]
+        def parking_place(gi):
+            first = min(GROUP * PADDED * gi, B * H * T * T - GROUP * PADDED)
+            return out_flat[first : first + GROUP * PADDED]
 
         def pad_rel(gi):
             nc.scalar.copy(
-                out=stg[gi % NSTG][:].rearrange("p (i c) -> p i c", i=GROUP)[:, :, 1 : T + 1],
-                in_=rels[gi][:].rearrange("p (i j) -> p i j", i=GROUP),
+                out=padded_tiles[gi % 3][:].rearrange("p (i c) -> p i c", i=GROUP)[:, :, 1 : T + 1],
+                in_=rel_banks[gi][:].rearrange("p (i j) -> p i j", i=GROUP),
             )
 
         def park(gi):
             nc.sync.dma_start(
-                out=area_of(gi).rearrange("(i t c) -> t i c", i=GROUP, t=T),
-                in_=stg[gi % NSTG][:].rearrange("p (i c) -> p i c", i=GROUP),
+                out=parking_place(gi).rearrange("(i t c) -> t i c", i=GROUP, t=T),
+                in_=padded_tiles[gi % 3][:].rearrange("p (i c) -> p i c", i=GROUP),
             )
 
-        def fetch(gi):
-            rb = back_pool.tile([P, GROUP * T], F32, tag="rb")
+        def fetch_shifted(gi):
+            back = results.tile([P, GROUP * T], F32, tag="shifted")
             nc.sync.dma_start(
-                out=rb[:].rearrange("p (i j) -> p i j", i=GROUP),
-                in_=area_of(gi).rearrange("(i f) -> i f", i=GROUP)[:, T:SLOT].rearrange("i (t j) -> t i j", t=T),
+                out=back[:].rearrange("p (i j) -> p i j", i=GROUP),
+                in_=parking_place(gi)
+                .rearrange("(i f) -> i f", i=GROUP)[:, T:PADDED]
+                .rearrange("i (t j) -> t i j", t=T),
             )
-            rbs[gi] = rb
+            shifted[gi] = back
 
         def final_add(gi):
-            fin = back_pool.tile([P, GROUP * T], F32, tag="fin")
-            nc.vector.tensor_tensor(out=fin[:], in0=conts[gi][:], in1=rbs[gi][:], op=ADD)
-            fins[gi] = fin
+            total = results.tile([P, GROUP * T], F32, tag="total")
+            nc.vector.tensor_tensor(out=total[:], in0=content_banks[gi][:], in1=shifted[gi][:], op=ADD)
+            finished[gi] = total
 
-        def final_store(gi):
+        def store(gi):
             nc.sync.dma_start(
                 out=out[2 * gi : 2 * gi + 2].rearrange("b h t j -> t (b h) j"),
-                in_=fins[gi][:].rearrange("p (i j) -> p i j", i=GROUP),
+                in_=finished[gi][:].rearrange("p (i j) -> p i j", i=GROUP),
             )
 
         groups = range(NGROUPS)
-        for s in range(-1, fa_step(NGROUPS - 1) + 1):
-            load_q(s + 1 + PF)
-            for b in range(PF, B):
-                if c_step(b) == s + 1 + PF:
+        for s in range(-1, final_step(NGROUPS - 1) + 1):
+            load_q(s + 1 + PREFETCH)
+            for b in range(PREFETCH, B):
+                if w_step(b) == s + 1 + PREFETCH:
                     load_k(b)
-            load_q_special(s + PERIOD + PF)
-            due = [gi for gi in groups if fa_step(gi) == s]
-            padded = [gi for gi in groups if 2 * gi + 3 == s]
-            for gi in due:
-                mult_content(gi)
-            for gi in padded:
-                pad_rel(gi)
-            next_k = [b for b in range(B) if c_step(b) == s + 1]
+            load_q_head1(s + SCALAR_PERIOD + PREFETCH)
+
+            for gi in groups:
+                if pad_step(gi) == s:
+                    pad_rel(gi)
+            next_k = [b for b in range(B) if w_step(b) == s + 1]
             if s >= 0:
                 for b in next_k:
-                    turn_k(b)
-            turn_special(s + PERIOD)
-            sums(s)
-            turn_q(s + 1)
+                    transpose_k(b)
+            add_biases(s)
+            transpose_q(s + 1, 0)
+            transpose_q_for_scalar(s + SCALAR_PERIOD)
+            transpose_q(s + 1, 1)
             if s == -1:
                 for b in next_k:
-                    turn_k(b)
-                prepare_r_tensor()
+                    transpose_k(b)
+                transpose_emb()
             if s == 1:
-                nc.vector.quantize_mx(out=rc[:].bitcast(FP8X4), scales=rs[:], in_=gr[:])
-            quants(s - 1)
-            mult_rel(s - 1)
-            offload(s)
-            for gi in due:
-                final_add(gi)
+                nc.vector.quantize_mx(out=emb_codes[:].bitcast(FP8X4), scales=emb_scales[:], in_=emb_grouped[:])
+            quantise_step(s - 1)
+            multiply_rel(s - 1)
+            scalar_adds(s)
             for gi in groups:
-                if 2 * gi + 4 == s:
-                    fetch(gi)
-            for gi in padded:
-                park(gi)
-            for gi in due:
-                final_store(gi)
+                if final_step(gi) == s:
+                    final_add(gi)
+            for gi in groups:
+                if final_step(gi) == s + 1:
+                    multiply_content(gi)
+
+            for gi in groups:
+                if pad_step(gi) + 1 == s:
+                    fetch_shifted(gi)
+            for gi in groups:
+                if pad_step(gi) == s:
+                    park(gi)
+            for gi in groups:
+                if final_step(gi) == s:
+                    store(gi)

from contextlib import ExitStack

import concourse.mybir as mybir
from concourse.masks import make_identity

F32 = mybir.dt.float32
BF16 = mybir.dt.bfloat16
U32 = mybir.dt.uint32
U8 = mybir.dt.uint8
FP8X4 = mybir.dt.float8_e4m3fn_x4
ADD = mybir.AluOpType.add
IDENTITY = mybir.ActivationFunctionType.Identity

B, T, H, D = 32, 128, 2, 1024
P = 128
FLOPS = 2 * 2 * B * H * T * T * D

WORDS = D // 2
CODES = D // 4
GROUP = 4
NGROUPS = B * H // GROUP
PADDED = (T + 1) * T

PREFETCH = 3
LATE = 4
EARLY = B - LATE
SCALAR_PERIOD = 3
SCALAR_ADDS = 16
FIRST_SCALAR_BATCH = SCALAR_PERIOD + PREFETCH


def made_by_scalar(b):
    return FIRST_SCALAR_BATCH <= b < EARLY and b % SCALAR_PERIOD == FIRST_SCALAR_BATCH % SCALAR_PERIOD


def w_step(b):
    return b if b < EARLY else b + LATE


def pad_step(gi):
    return 2 * gi + 3


def final_step(gi):
    s = pad_step(gi)
    halves = 2 if s < EARLY else 1
    while halves < 5:
        s += 1
        halves += 2 if s < EARLY else 1
    return max(s, w_step(2 * gi + 1) + 2)


def transpose_matrix(nc, bank, words, identity):
    for u in range(2):
        for g in range(2):
            block = 2 * u + g
            first = 256 * g + 128 * u
            nc.tensor.transpose(bank[:, P * block : P * block + P], words[:, first : first + P], identity)


def copy_regrouped(nc, dst_words, bank):
    nc.scalar.copy(
        out=dst_words.rearrange("p (x u) -> p x u", u=2),
        in_=bank[:].rearrange("p (u x) -> p x u", u=2),
    )


def multiply_batch(nc, bank, b, left, right):
    left_codes, left_scales, left_first = left
    right_codes, right_scales, right_first = right
    for h in range(H):
        matrix = H * (b % 2) + h
        for g in range(2):
            lo = left_first + P * (2 * h + g)
            ro = right_first + P * (2 * h + g)
            nc.tensor.matmul_mx(
                out=bank[:, T * matrix : T * matrix + T],
                lhsT=left_codes[:, lo : lo + P].bitcast(FP8X4),
                lhsT_scale=left_scales[:, lo : lo + P],
                rhs=right_codes[:, ro : ro + P].bitcast(FP8X4),
                rhs_scale=right_scales[:, ro : ro + P],
                start=(g == 0),
                stop=(g == 1),
            )


def tile_relativepositionembedding_pa_t_kernel(tc, q, k, r_w_bias, r_r_bias, rel_pos_emb, out):
    nc = tc.nc
    out_flat = out.rearrange("b h t j -> (b h t j)")
    with ExitStack() as ctx:
        const = ctx.enter_context(tc.tile_pool(name="const", bufs=1))
        loads = ctx.enter_context(tc.tile_pool(name="loads", bufs=PREFETCH + 2))
        kept = ctx.enter_context(tc.tile_pool(name="kept", bufs=LATE + 1))
        sums_pool = ctx.enter_context(tc.tile_pool(name="sums", bufs=3))
        codes = ctx.enter_context(tc.tile_pool(name="codes", bufs=7))
        results = ctx.enter_context(tc.tile_pool(name="results", bufs=3))
        psum = ctx.enter_context(tc.psum_pool(name="psum", bufs=2))
        ctx.enter_context(tc.manual_schedule())

        identity = const.tile([P, P], F32)
        make_identity(nc, identity[:])

        bias_rows = const.tile([P, D], BF16)
        nc.vector.memset(bias_rows[:], 0.0)
        nc.sync.dma_start(out=bias_rows[0:H, :], in_=r_w_bias)
        nc.sync.dma_start(out=bias_rows[H : 2 * H, :], in_=r_r_bias)

        q_tiles = {}
        q_head1_tiles = {}
        k_tiles = {}

        def load_q(b):
            if not 0 <= b < B:
                return
            q_tile = loads.tile([P, H * D], BF16, tag="q")
            if made_by_scalar(b):
                nc.sync.dma_start(out=q_tile[:, 0:D], in_=q[b][:, 0, :])
            elif b == 0:
                for h in range(H):
                    nc.sync.dma_start(out=q_tile[:, D * h : D * h + D], in_=q[b][:, h, :])
            else:
                nc.sync.dma_start(out=q_tile[:], in_=q[b].rearrange("t h d -> t (h d)"))
            q_tiles[b] = q_tile

        def load_q_head1(b):
            if made_by_scalar(b):
                q_head1 = loads.tile([P, D], BF16, tag="q_head1", bufs=2)
                nc.sync.dma_start(out=q_head1[:], in_=q[b][:, 1, :])
                q_head1_tiles[b] = q_head1

        def load_k(b):
            k_tile = loads.tile([P, H * D], BF16, tag="k")
            nc.sync.dma_start(out=k_tile[:], in_=k[b].rearrange("t h d -> t (h d)"))
            k_tiles[b] = k_tile

        load_q(0)
        load_k(0)
        emb_rows = const.tile([P, H * D], BF16)
        nc.sync.dma_start(out=emb_rows[:], in_=rel_pos_emb.rearrange("j h d -> j (h d)"))
        for b in range(1, PREFETCH):
            load_q(b)
            load_k(b)

        padded_tiles = []
        for n in range(3):
            padded = const.tile([P, GROUP * (T + 1)], F32, name="padded%d" % n)
            nc.vector.memset(padded[:], 0.0)
            padded_tiles.append(padded)

        bias_bank = psum.tile([P, WORDS], F32, tag="k_bank")
        bias_words = bias_rows[:].bitcast(F32)
        for c in range(4):
            nc.tensor.transpose(bias_bank[:, P * c : P * c + P], bias_words[:, P * c : P * c + P], identity[:])
        bias_small = const.tile([P, 16], F32)
        nc.vector.tensor_copy(
            out=bias_small[:].rearrange("p (i c) -> p i c", c=4),
            in_=bias_bank[:].rearrange("p (c i) -> p i c", c=4)[:, 0:4, :],
        )
        bias_wide = const.tile([P, 4 * D], BF16, align_bytes=64)
        bias_wide_words = bias_wide[:].bitcast(F32)
        for i in (2, 0, 3, 1):
            nc.vector.tensor_copy(
                out=bias_wide_words[:, WORDS * i : WORDS * i + WORDS].rearrange("p (g r u) -> p g r u", g=2, u=2),
                in_=bias_small[:, 4 * i : 4 * i + 4]
                .rearrange("p (g u) -> p g u", g=2)
                .unsqueeze(2)
                .to_broadcast([P, 2, T, 2]),
            )
        bias_f32 = const.tile([P, 32], F32)
        nc.vector.tensor_copy(out=bias_f32[:], in_=bias_small[:].bitcast(BF16))

        emb_grouped = const.tile([P, H * D], BF16, align_bytes=64)
        emb_codes = const.tile([P, H * CODES], U32, align_bytes=64)
        emb_scales = const.tile([P, H * CODES], U8, align_bytes=64)

        def transpose_emb():
            for h in range(H):
                bank = psum.tile([P, WORDS], F32, tag="k_bank")
                transpose_matrix(nc, bank, emb_rows[:].bitcast(F32)[:, WORDS * h : WORDS * h + WORDS], identity[:])
                copy_regrouped(nc, emb_grouped[:].bitcast(F32)[:, WORDS * h : WORDS * h + WORDS], bank)

        q_banks = {}
        scalar_banks = {}
        kept_q = {}
        k_grouped = {}
        sum_tiles = {}
        code_of = {}
        rel_banks = {}
        content_banks = {}
        shifted = {}
        finished = {}

        def transpose_q(b, h):
            if not 0 <= b < B or (h == 1 and made_by_scalar(b)):
                return
            bank = psum.tile([P, WORDS], F32, tag="q_bank")
            transpose_matrix(nc, bank, q_tiles[b][:].bitcast(F32)[:, WORDS * h : WORDS * h + WORDS], identity[:])
            if b < EARLY:
                q_banks[(b, h)] = bank
                return
            if h == 0:
                kept_tile = kept.tile([P, H * WORDS], F32, tag="kept_q")
                kept_q[b] = kept_tile
            copy_regrouped(nc, kept_q[b][:, WORDS * h : WORDS * h + WORDS], bank)

        def transpose_q_for_scalar(b):
            if made_by_scalar(b):
                bank = psum.tile([P, WORDS], F32, tag="scalar_bank")
                transpose_matrix(nc, bank, q_head1_tiles[b][:].bitcast(F32), identity[:])
                scalar_banks[b] = bank
                early_sums = sums_pool.tile([P, 4 * D], BF16, tag="sums_scalar", bufs=2, align_bytes=64)
                sum_tiles[b] = early_sums

        def transpose_k(b):
            grouped = sums_pool.tile([P, H * D], BF16, tag="k_grouped", align_bytes=64)
            for h in range(H):
                bank = psum.tile([P, WORDS], F32, tag="k_bank")
                transpose_matrix(nc, bank, k_tiles[b][:].bitcast(F32)[:, WORDS * h : WORDS * h + WORDS], identity[:])
                copy_regrouped(nc, grouped[:].bitcast(F32)[:, WORDS * h : WORDS * h + WORDS], bank)
            k_grouped[b] = grouped

        def bias_row(bias, h):
            return H * (1 - bias) + h

        def add_biases(s):
            if 0 <= s < EARLY:
                if not made_by_scalar(s):
                    both_sums = sums_pool.tile([P, 4 * D], BF16, tag="sums", align_bytes=64)
                    sum_tiles[s] = both_sums
                for h in range(H):
                    if h == 1 and made_by_scalar(s):
                        continue
                    bank = q_banks[(s, h)][:].bitcast(BF16).rearrange("p (u x e) -> p x u e", u=2, e=2)
                    for bias in range(2):
                        at = D * (H * bias + h)
                        row = D * bias_row(bias, h)
                        nc.vector.tensor_tensor(
                            out=sum_tiles[s][:, at : at + D].rearrange("p (x u e) -> p x u e", u=2, e=2),
                            in0=bank,
                            in1=bias_wide[:, row : row + D].rearrange("p (x u e) -> p x u e", u=2, e=2),
                            op=ADD,
                        )
            for bias, b in ((0, s), (1, s - LATE)):
                if EARLY <= b < B:
                    one_sum = sums_pool.tile([P, 4 * D], BF16, tag="sums", align_bytes=64)
                    row = D * bias_row(bias, 0)
                    nc.vector.tensor_tensor(
                        out=one_sum[:, 0 : H * D],
                        in0=kept_q[b][:].bitcast(BF16),
                        in1=bias_wide[:, row : row + H * D],
                        op=ADD,
                    )
                    sum_tiles[(bias, b)] = one_sum

        def scalar_adds(s):
            for b in range(s + 1, s + SCALAR_PERIOD + 1):
                if not made_by_scalar(b):
                    continue
                part = s - (b - SCALAR_PERIOD)
                bank = scalar_banks[b][:].bitcast(BF16).rearrange("p (c r e) -> p c r e", c=4, e=2)
                for n in range(SCALAR_ADDS * part // SCALAR_PERIOD, SCALAR_ADDS * (part + 1) // SCALAR_PERIOD):
                    bias, g, u, e = n // 8, n // 4 % 2, n // 2 % 2, n % 2
                    at = D * (H * bias + 1) + 512 * g
                    column = 8 * bias_row(bias, 1) + 4 * g + 2 * u + e
                    nc.scalar.activation(
                        out=sum_tiles[b][:, at : at + 512].rearrange("p (r j) -> p r j", j=4)[:, :, 2 * u + e],
                        in_=bank[:, 2 * u + g, :, e],
                        func=IDENTITY,
                        bias=bias_f32[:, column : column + 1],
                        scale=1.0,
                    )

        def quantise_sums(src, width):
            packed = codes.tile([P, 4 * CODES], U32, tag="q_codes", align_bytes=64)
            scales = codes.tile([P, 4 * CODES], U8, tag="q_scales", align_bytes=64)
            nc.vector.quantize_mx(
                out=packed[:, 0 : width // 4].bitcast(FP8X4), scales=scales[:, 0 : width // 4], in_=src[:, 0:width]
            )
            return packed, scales

        def quantise_k(b):
            packed = codes.tile([P, H * CODES], U32, tag="k_codes", align_bytes=64)
            scales = codes.tile([P, H * CODES], U8, tag="k_scales", align_bytes=64)
            nc.vector.quantize_mx(out=packed[:].bitcast(FP8X4), scales=scales[:], in_=k_grouped[b][:])
            code_of[("k", b)] = (packed, scales, 0)

        def quantise_step(s):
            if 0 <= s < EARLY:
                packed, scales = quantise_sums(sum_tiles[s], 4 * D)
                code_of[("q+r_r", s)] = (packed, scales, 0)
                code_of[("q+r_w", s)] = (packed, scales, H * CODES)
                quantise_k(s)
            if EARLY <= s < B:
                packed, scales = quantise_sums(sum_tiles[(0, s)], H * D)
                code_of[("q+r_r", s)] = (packed, scales, 0)
            if EARLY <= s - LATE < B:
                packed, scales = quantise_sums(sum_tiles[(1, s - LATE)], H * D)
                code_of[("q+r_w", s - LATE)] = (packed, scales, 0)
                quantise_k(s - LATE)

        def multiply_rel(b):
            if 0 <= b < B:
                if b % 2 == 0:
                    rel_bank = psum.tile([P, GROUP * T], F32, tag="rel", bufs=1)
                    rel_banks[b // 2] = rel_bank
                multiply_batch(nc, rel_banks[b // 2], b, code_of[("q+r_r", b)], (emb_codes, emb_scales, 0))

        def multiply_content(gi):
            content_bank = psum.tile([P, GROUP * T], F32, tag="content", bufs=1)
            for b in (2 * gi, 2 * gi + 1):
                multiply_batch(nc, content_bank, b, code_of[("q+r_w", b)], code_of[("k", b)])
            content_banks[gi] = content_bank

        def parking_place(gi):
            first = min(GROUP * PADDED * gi, B * H * T * T - GROUP * PADDED)
            return out_flat[first : first + GROUP * PADDED]

        def pad_rel(gi):
            nc.scalar.copy(
                out=padded_tiles[gi % 3][:].rearrange("p (i c) -> p i c", i=GROUP)[:, :, 1 : T + 1],
                in_=rel_banks[gi][:].rearrange("p (i j) -> p i j", i=GROUP),
            )

        def park(gi):
            nc.sync.dma_start(
                out=parking_place(gi).rearrange("(i t c) -> t i c", i=GROUP, t=T),
                in_=padded_tiles[gi % 3][:].rearrange("p (i c) -> p i c", i=GROUP),
            )

        def fetch_shifted(gi):
            back = results.tile([P, GROUP * T], F32, tag="shifted")
            nc.sync.dma_start(
                out=back[:].rearrange("p (i j) -> p i j", i=GROUP),
                in_=parking_place(gi)
                .rearrange("(i f) -> i f", i=GROUP)[:, T:PADDED]
                .rearrange("i (t j) -> t i j", t=T),
            )
            shifted[gi] = back

        def final_add(gi):
            total = results.tile([P, GROUP * T], F32, tag="total")
            nc.vector.tensor_tensor(out=total[:], in0=content_banks[gi][:], in1=shifted[gi][:], op=ADD)
            finished[gi] = total

        def store(gi):
            nc.sync.dma_start(
                out=out[2 * gi : 2 * gi + 2].rearrange("b h t j -> t (b h) j"),
                in_=finished[gi][:].rearrange("p (i j) -> p i j", i=GROUP),
            )

        groups = range(NGROUPS)
        for s in range(-1, final_step(NGROUPS - 1) + 1):
            load_q(s + 1 + PREFETCH)
            for b in range(PREFETCH, B):
                if w_step(b) == s + 1 + PREFETCH:
                    load_k(b)
            load_q_head1(s + SCALAR_PERIOD + PREFETCH)

            for gi in groups:
                if pad_step(gi) == s:
                    pad_rel(gi)
            next_k = [b for b in range(B) if w_step(b) == s + 1]
            if s >= 0:
                for b in next_k:
                    transpose_k(b)
            add_biases(s)
            transpose_q(s + 1, 0)
            transpose_q_for_scalar(s + SCALAR_PERIOD)
            transpose_q(s + 1, 1)
            if s == -1:
                for b in next_k:
                    transpose_k(b)
                transpose_emb()
            if s == 1:
                nc.vector.quantize_mx(out=emb_codes[:].bitcast(FP8X4), scales=emb_scales[:], in_=emb_grouped[:])
            quantise_step(s - 1)
            multiply_rel(s - 1)
            scalar_adds(s)
            for gi in groups:
                if final_step(gi) == s:
                    final_add(gi)
            for gi in groups:
                if final_step(gi) == s + 1:
                    multiply_content(gi)

            for gi in groups:
                if pad_step(gi) + 1 == s:
                    fetch_shifted(gi)
            for gi in groups:
                if pad_step(gi) == s:
                    park(gi)
            for gi in groups:
                if final_step(gi) == s:
                    store(gi)
